import numpy as np
import ml_dtypes


def mxq(x, axis, fmt="e4m3"):
    dtype, down = {"e4m3": (ml_dtypes.float8_e4m3fn, 7), "e5m2": (ml_dtypes.float8_e5m2, 14)}[fmt]
    v = np.moveaxis(np.asarray(x, np.float32).astype(ml_dtypes.bfloat16).astype(np.float64), axis, -1)
    blocks = v.reshape(v.shape[:-1] + (-1, 32))
    amax = np.abs(blocks).max(-1, keepdims=True)
    byte = np.maximum(np.where(amax > 0, np.frexp(amax)[1] - 1 + 127, 0) - down, 1)
    scale = np.exp2(byte - 127.0)
    codes = (blocks / scale).astype(np.float32).astype(dtype).astype(np.float64)
    return np.moveaxis((codes * scale).reshape(v.shape), -1, axis)


WIDE = False


def mx_kscale(k):
    if not WIDE:
        return np.ones(k)
    levels = np.array([10, -10, 5, -5, 0])
    a = np.random.permutation(np.resize(levels, k // 512 * 4)).reshape(k // 512, 4)
    idx = np.arange(k)
    return np.exp2(a[idx // 512, idx % 128 // 32])


BF16 = ml_dtypes.bfloat16


def bf(x):
    return np.asarray(x, np.float32).astype(BF16)


def f64(x):
    return np.asarray(x).astype(np.float64)


B, F, G, N, L = 64, 512, 128, 100, 7
S2 = (L + 1) ** 2


def setup_inputs():
    s = mx_kscale(F)
    return {"x": bf(np.random.standard_normal((B, F, S2)) * s[None, :, None]),
            "psi": bf(np.random.standard_normal((G, F, S2)) / s[None, :, None])}


def reference(x, psi):
    xq = mxq(f64(x), 1, "e4m3")
    pq = mxq(f64(psi), 1, "e4m3")
    scale = 1.0 / np.sqrt(F)
    outs = []
    for l in range(L + 1):
        s, d = l * l, 2 * l + 1
        a = xq[:, :, s:s + d].transpose(0, 2, 1).reshape(B * d, F)
        p = pq[:, :, s:s + d].transpose(1, 0, 2).reshape(F, G * d)
        o = scale * (a @ p)
        outs.append(o.reshape(B, d, G, d).transpose(2, 0, 1, 3).reshape(G, B, d * d))
    return np.concatenate(outs, axis=-1)

@@ -1,0 +1,181 @@
+from contextlib import ExitStack
+
+import concourse.bass as bass
+import concourse.mybir as mybir
+import concourse.tile as tile
+
+FP8X4 = mybir.dt.float8_e4m3fn_x4
+BF16 = mybir.dt.bfloat16
+F32 = mybir.dt.float32
+U32 = mybir.dt.uint32
+U8 = mybir.dt.uint8
+I32 = mybir.dt.int32
+
+P = 128
+B, F, G, S2, LMAX = 64, 512, 128, 64, 7
+C = 680
+GL = 16
+NCHUNK = 4
+SCALE = 1.0 / (512.0 ** 0.5)
+FLOPS = 2 * F * B * G * C
+VSPLIT = 176
+
+
+def c_of(l):
+    return sum((2 * k + 1) ** 2 for k in range(l))
+
+
+def u_groups(l):
+    d = 2 * l + 1
+    per = 2 if l >= 4 else 4
+    cuts = [0, d]
+    for u in range(1, d):
+        if c_of(l) + u * d == VSPLIT:
+            cuts.append(u)
+    cuts = sorted(cuts)
+    groups = []
+    for a, b in zip(cuts[:-1], cuts[1:]):
+        for u0 in range(a, b, per):
+            groups.append((u0, min(u0 + per, b)))
+    return groups
+
+
+def tile_s2conv_pa_kernel(tc, x, psi, out):
+    nc = tc.nc
+    x_v = x.rearrange("b (p t) s -> p b (t s)", t=4)
+    psi_v = psi.rearrange("g (p t) s -> p g (t s)", t=4)
+    out_v = out.flatten_outer_dims().rearrange("(gl p) c -> p gl c", p=P)
+
+    with ExitStack() as ctx:
+        keep = ctx.enter_context(tc.tile_pool(name="keep", bufs=1))
+        rawp = ctx.enter_context(tc.tile_pool(name="rawp", bufs=3))
+        gpool = ctx.enter_context(tc.tile_pool(name="gpool", bufs=2))
+        opool = ctx.enter_context(tc.tile_pool(name="opool", bufs=2))
+        psum = ctx.enter_context(tc.psum_pool(name="psum", bufs=8))
+
+        xc = keep.tile([P, 64 + 128 * S2], U32, name="xc", align_bytes=64)
+        xs = keep.tile([P, 64 + 128 * S2], U8, name="xs", align_bytes=64)
+        xci = xc[:].bitcast(I32)
+        xsi = xs[:].bitcast(I32)
+        nc.vector.memset(xci[:, 0:8192].rearrange("p (k w) -> p k w", w=128)[:, :, 0:64], 0)
+        nc.vector.memset(xci[:, 8192:8256], 0)
+        nc.vector.memset(xsi[:, 0:2048].rearrange("p (k w) -> p k w", w=32)[:, :, 0:16], 0)
+        nc.vector.memset(xsi[:, 2048:2064], 0)
+
+        def load_psi(c):
+            raw = rawp.tile([P, 32, 256], BF16, name="raw", tag="raw")
+            nc.sync.dma_start(out=raw[:], in_=psi_v[:, 32 * c:32 * c + 32, :])
+            return raw
+
+        def prep_psi(raw, skew):
+            gp = gpool.tile([P, 4, 2, 256, 4], BF16, name="gp", tag="gp", align_bytes=64)
+            pc = gpool.tile([P, 4, 2, 256], U32, name="pc", tag="pc", align_bytes=64)
+            ps = gpool.tile([P, 4, 2, 256], U8, name="ps", tag="ps", align_bytes=64)
+            rv = raw[:].rearrange("p (gl h) (t s) -> p h gl t s", h=2, t=4)
+
+            def regroup(j):
+                for l, off in ((7 - j, 0), (j, GL * (15 - 2 * j))):
+                    d = 2 * l + 1
+                    s0 = l * l
+                    for h in range(2):
+                        nc.vector.tensor_copy(
+                            out=gp[:, j, h, off:off + GL * d, :].rearrange("p (gl m) t -> p gl m t", m=d),
+                            in_=rv[:, h, :, :, s0:s0 + d].rearrange("p gl t m -> p gl m t"),
+                        )
+
+            def quant(j):
+                nc.vector.quantize_mx(
+                    out=pc[:, j].rearrange("p h w -> p (h w)").bitcast(FP8X4),
+                    scales=ps[:, j].rearrange("p h w -> p (h w)"),
+                    in_=gp[:, j].rearrange("p h w t -> p (h w t)"),
+                )
+
+            if skew:
+                regroup(0)
+                for j in range(1, 4):
+                    regroup(j)
+                    quant(j - 1)
+                quant(3)
+            else:
+                for j in range(4):
+                    regroup(j)
+                    quant(j)
+            return pc, ps
+
+        raw0 = load_psi(0)
+        xr = []
+        for i in range(2):
+            xraw = rawp.tile([P, 32, 256], BF16, name="xraw", tag="raw")
+            xr.append(xraw)
+        pieces = [(0, 16), (16, 16), (32, 16), (48, 8), (56, 8)]
+        for b0, nb in pieces:
+            t = xr[b0 // 32]
+            nc.sync.dma_start(out=t[:, b0 % 32:b0 % 32 + nb, :], in_=x_v[:, b0:b0 + nb, :])
+
+        pcs = prep_psi(raw0, False)
+
+        xg = opool.tile([P, S2, B, 4], BF16, name="xg", tag="o", align_bytes=64)
+        for b0, nb in pieces:
+            t = xr[b0 // 32]
+            nv = 12 if nb == 16 else 4
+            for eng, a, n in (("v", b0, nv), ("s", b0 + nv, nb - nv)):
+                src = t[:, a % 32:a % 32 + n, :].rearrange("p b (t s) -> p b s t", t=4)
+                dst = xg[:, :, a:a + n, :].rearrange("p s b t -> p b s t")
+                if eng == "v":
+                    nc.vector.tensor_copy(out=dst, in_=src)
+                else:
+                    nc.scalar.copy(out=dst, in_=src)
+        for s in reversed(range(S2)):
+            lo = 128 * s + 64
+            nc.vector.quantize_mx(
+                out=xc[:, lo:lo + 64].bitcast(FP8X4),
+                scales=xs[:, lo:lo + 64],
+                in_=xg[:, s].rearrange("p b t -> p (b t)"),
+            )
+
+        raws = {1: load_psi(1)}
+        for c in range(NCHUNK):
+            pc, ps = pcs
+            if c + 2 < NCHUNK:
+                raws[c + 2] = load_psi(c + 2)
+            if c + 1 < NCHUNK:
+                pcs = prep_psi(raws[c + 1], True)
+            o = opool.tile([P, GL, C], F32, name="o", tag="o", align_bytes=64)
+            last = c == NCHUNK - 1
+            done_to = C
+            for l in range(LMAX, -1, -1):
+                d = 2 * l + 1
+                s0 = l * l
+                cl = c_of(l)
+                if l >= 4:
+                    j, n, w0, off = 7 - l, 256, 0, 0
+                else:
+                    j, n, w0, off = l, 128, 128, GL * (15 - 2 * l) - 128
+                for u0, u1 in u_groups(l):
+                    acc = psum.tile([P, 512], F32, name="acc", tag="acc")
+                    for i, u in enumerate(range(u0, u1)):
+                        s = s0 + u
+                        for h in range(2):
+                            lo = 128 * s + 64 - 64 * h
+                            nc.tensor.matmul_mx(
+                                out=acc[:, i * n:(i + 1) * n],
+                                lhsT=xc[:, lo:lo + 128].bitcast(FP8X4),
+                                lhsT_scale=xs[:, lo:lo + 128],
+                                rhs=pc[:, j, h, w0:w0 + n].bitcast(FP8X4),
+                                rhs_scale=ps[:, j, h, w0:w0 + n],
+                                start=(h == 0),
+                                stop=(h == 1),
+                            )
+                    nu = u1 - u0
+                    src = acc[:, 0:nu * n].rearrange("p (u n) -> p u n", n=n)[:, :, off:off + GL * d]
+                    src = src.rearrange("p u (g m) -> p g u m", m=d)
+                    dst = o[:, :, cl + u0 * d:cl + u1 * d].rearrange("p g (u m) -> p g u m", m=d)
+                    if cl + u0 * d < VSPLIT:
+                        nc.vector.tensor_scalar_mul(out=dst, in0=src, scalar1=SCALE)
+                    else:
+                        nc.scalar.activation(out=dst, in_=src, func=mybir.ActivationFunctionType.Copy, scale=SCALE)
+                if last and l >= 4:
+                    lo_c = (cl + 7) // 8 * 8
+                    nc.sync.dma_start(out=out_v[:, GL * c:GL * c + GL, lo_c:done_to], in_=o[:, :, lo_c:done_to])
+                    done_to = lo_c
+            nc.sync.dma_start(out=out_v[:, GL * c:GL * c + GL, 0:done_to], in_=o[:, :, 0:done_to])

@@ -43,14 +43,14 @@ def u_groups(l):
 def tile_s2conv_pa_kernel(tc, x, psi, out):
     nc = tc.nc
     x_v = x.rearrange("b (p t) s -> p b (t s)", t=4)
-    psi_v = psi.rearrange("g (p t) s -> p g (t s)", t=4)
+    psi_v = psi.rearrange("(gl h) (p t) s -> h p gl (t s)", h=2, t=4)
     out_v = out.flatten_outer_dims().rearrange("(gl p) c -> p gl c", p=P)
 
     with ExitStack() as ctx:
         keep = ctx.enter_context(tc.tile_pool(name="keep", bufs=1))
-        rawp = ctx.enter_context(tc.tile_pool(name="rawp", bufs=3))
+        rawp = ctx.enter_context(tc.tile_pool(name="rawp", bufs=4))
         gpool = ctx.enter_context(tc.tile_pool(name="gpool", bufs=2))
-        opool = ctx.enter_context(tc.tile_pool(name="opool", bufs=2))
+        opool = ctx.enter_context(tc.tile_pool(name="opool", bufs=3))
         psum = ctx.enter_context(tc.psum_pool(name="psum", bufs=8))
 
         xc = keep.tile([P, 64 + 128 * S2], U32, name="xc", align_bytes=64)
@@ -62,69 +62,72 @@ def tile_s2conv_pa_kernel(tc, x, psi, out):
         nc.vector.memset(xsi[:, 0:2048].rearrange("p (k w) -> p k w", w=32)[:, :, 0:16], 0)
         nc.vector.memset(xsi[:, 2048:2064], 0)
 
-        def load_psi(c):
-            raw = rawp.tile([P, 32, 256], BF16, name="raw", tag="raw")
-            nc.sync.dma_start(out=raw[:], in_=psi_v[:, 32 * c:32 * c + 32, :])
-            return raw
+        order = [("p", 0, 0), ("p", 0, 1), ("x", 0, 0), ("x", 16, 0), ("x", 32, 0), ("x", 48, 0)]
+        for c in range(1, NCHUNK):
+            order.extend([("p", c, 0), ("p", c, 1)])
+        loaded = {}
+        state = {"next": 0}
 
-        def prep_psi(raw, skew):
-            gp = gpool.tile([P, 4, 2, 256, 4], BF16, name="gp", tag="gp", align_bytes=64)
-            pc = gpool.tile([P, 4, 2, 256], U32, name="pc", tag="pc", align_bytes=64)
-            ps = gpool.tile([P, 4, 2, 256], U8, name="ps", tag="ps", align_bytes=64)
-            rv = raw[:].rearrange("p (gl h) (t s) -> p h gl t s", h=2, t=4)
-
-            def regroup(j):
-                for l, off in ((7 - j, 0), (j, GL * (15 - 2 * j))):
-                    d = 2 * l + 1
-                    s0 = l * l
-                    for h in range(2):
-                        nc.vector.tensor_copy(
-                            out=gp[:, j, h, off:off + GL * d, :].rearrange("p (gl m) t -> p gl m t", m=d),
-                            in_=rv[:, h, :, :, s0:s0 + d].rearrange("p gl t m -> p gl m t"),
-                        )
-
-            def quant(j):
-                nc.vector.quantize_mx(
-                    out=pc[:, j].rearrange("p h w -> p (h w)").bitcast(FP8X4),
-                    scales=ps[:, j].rearrange("p h w -> p (h w)"),
-                    in_=gp[:, j].rearrange("p h w t -> p (h w t)"),
-                )
-
-            if skew:
-                regroup(0)
-                for j in range(1, 4):
-                    regroup(j)
-                    quant(j - 1)
-                quant(3)
+        def load_next():
+            k = state["next"]
+            if k >= len(order):
+                return
+            state["next"] = k + 1
+            kind, a, h = order[k]
+            raw = rawp.tile([P, 16, 256], BF16, name="raw", tag="raw")
+            if kind == "p":
+                nc.sync.dma_start(out=raw[:], in_=psi_v[h][:, GL * a:GL * a + GL, :])
+            elif a == 48:
+                nc.sync.dma_start(out=raw[:, 0:8, :], in_=x_v[:, a:a + 8, :])
+                nc.sync.dma_start(out=raw[:, 8:16, :], in_=x_v[:, a + 8:a + 16, :])
             else:
+                nc.sync.dma_start(out=raw[:], in_=x_v[:, a:a + 16, :])
+            loaded[order[k]] = raw
+
+        for k in range(4):
+            load_next()
+
+        def prep_psi(c):
+            pc = gpool.tile([P, 2, 1024], U32, name="pc", tag="pc", align_bytes=64)
+            ps = gpool.tile([P, 2, 1024], U8, name="ps", tag="ps", align_bytes=64)
+            for h in range(2):
+                raw = loaded[("p", c, h)]
+                gp = gpool.tile([P, 4, 256, 4], BF16, name="gp", tag="gp", align_bytes=64)
+                rv = raw[:].rearrange("p gl (t s) -> p gl t s", t=4)
                 for j in range(4):
-                    regroup(j)
-                    quant(j)
+                    for l, off in ((7 - j, 0), (j, GL * (15 - 2 * j))):
+                        d = 2 * l + 1
+                        s0 = l * l
+                        nc.vector.tensor_copy(
+                            out=gp[:, j, off:off + GL * d, :].rearrange("p (gl m) t -> p gl m t", m=d),
+                            in_=rv[:, :, :, s0:s0 + d].rearrange("p gl t m -> p gl m t"),
+                        )
+                load_next()
+                for q in range(2):
+                    nc.vector.quantize_mx(
+                        out=pc[:, h, 512 * q:512 * q + 512].bitcast(FP8X4),
+                        scales=ps[:, h, 512 * q:512 * q + 512],
+                        in_=gp[:, 2 * q:2 * q + 2].rearrange("p j w t -> p (j w t)"),
+                    )
             return pc, ps
 
-        raw0 = load_psi(0)
-        xr = []
-        for i in range(2):
-            xraw = rawp.tile([P, 32, 256], BF16, name="xraw", tag="raw")
-            xr.append(xraw)
-        pieces = [(0, 16), (16, 16), (32, 16), (48, 8), (56, 8)]
-        for b0, nb in pieces:
-            t = xr[b0 // 32]
-            nc.sync.dma_start(out=t[:, b0 % 32:b0 % 32 + nb, :], in_=x_v[:, b0:b0 + nb, :])
-
-        pcs = prep_psi(raw0, False)
+        pcs = prep_psi(0)
 
         xg = opool.tile([P, S2, B, 4], BF16, name="xg", tag="o", align_bytes=64)
-        for b0, nb in pieces:
-            t = xr[b0 // 32]
-            nv = 12 if nb == 16 else 4
-            for eng, a, n in (("v", b0, nv), ("s", b0 + nv, nb - nv)):
-                src = t[:, a % 32:a % 32 + n, :].rearrange("p b (t s) -> p b s t", t=4)
-                dst = xg[:, :, a:a + n, :].rearrange("p s b t -> p b s t")
+        for b0 in (0, 16, 32, 48):
+            raw = loaded[("x", b0, 0)]
+            if b0 == 48:
+                parts = (("v", 0, 4), ("s", 4, 4), ("v", 8, 4), ("s", 12, 4))
+            else:
+                parts = (("v", 0, 12), ("s", 12, 4))
+            for eng, a, n in parts:
+                src = raw[:, a:a + n, :].rearrange("p b (t s) -> p b s t", t=4)
+                dst = xg[:, :, b0 + a:b0 + a + n, :].rearrange("p s b t -> p b s t")
                 if eng == "v":
                     nc.vector.tensor_copy(out=dst, in_=src)
                 else:
                     nc.scalar.copy(out=dst, in_=src)
+            load_next()
         for s in reversed(range(S2)):
             lo = 128 * s + 64
             nc.vector.quantize_mx(
@@ -133,13 +136,10 @@ def tile_s2conv_pa_kernel(tc, x, psi, out):
                 in_=xg[:, s].rearrange("p b t -> p (b t)"),
             )
 
-        raws = {1: load_psi(1)}
         for c in range(NCHUNK):
             pc, ps = pcs
-            if c + 2 < NCHUNK:
-                raws[c + 2] = load_psi(c + 2)
             if c + 1 < NCHUNK:
-                pcs = prep_psi(raws[c + 1], True)
+                pcs = prep_psi(c + 1)
             o = opool.tile([P, GL, C], F32, name="o", tag="o", align_bytes=64)
             last = c == NCHUNK - 1
             done_to = C
@@ -151,6 +151,7 @@ def tile_s2conv_pa_kernel(tc, x, psi, out):
                     j, n, w0, off = 7 - l, 256, 0, 0
                 else:
                     j, n, w0, off = l, 128, 128, GL * (15 - 2 * l) - 128
+                w0 = w0 + 256 * j
                 for u0, u1 in u_groups(l):
                     acc = psum.tile([P, 512], F32, name="acc", tag="acc")
                     for i, u in enumerate(range(u0, u1)):
@@ -161,8 +162,8 @@ def tile_s2conv_pa_kernel(tc, x, psi, out):
                                 out=acc[:, i * n:(i + 1) * n],
                                 lhsT=xc[:, lo:lo + 128].bitcast(FP8X4),
                                 lhsT_scale=xs[:, lo:lo + 128],
-                                rhs=pc[:, j, h, w0:w0 + n].bitcast(FP8X4),
-                                rhs_scale=ps[:, j, h, w0:w0 + n],
+                                rhs=pc[:, h, w0:w0 + n].bitcast(FP8X4),
+                                rhs_scale=ps[:, h, w0:w0 + n],
                                 start=(h == 0),
                                 stop=(h == 1),
                             )
@@ -174,7 +175,7 @@ def tile_s2conv_pa_kernel(tc, x, psi, out):
                         nc.vector.tensor_scalar_mul(out=dst, in0=src, scalar1=SCALE)
                     else:
                         nc.scalar.activation(out=dst, in_=src, func=mybir.ActivationFunctionType.Copy, scale=SCALE)
-                if last and l >= 4:
+                if last and l == 5:
                     lo_c = (cl + 7) // 8 * 8
                     nc.sync.dma_start(out=out_v[:, GL * c:GL * c + GL, lo_c:done_to], in_=o[:, :, lo_c:done_to])
                     done_to = lo_c

@@ -18,6 +18,7 @@ GL = 16
 NCHUNK = 4
 SCALE = 1.0 / (512.0 ** 0.5)
 FLOPS = 2 * F * B * G * C
+TAIL = 176
 VSPLIT = 176
 
 
@@ -140,9 +141,14 @@ def tile_s2conv_pa_kernel(tc, x, psi, out):
             pc, ps = pcs
             if c + 1 < NCHUNK:
                 pcs = prep_psi(c + 1)
-            o = opool.tile([P, GL, C], F32, name="o", tag="o", align_bytes=64)
             last = c == NCHUNK - 1
-            done_to = C
+            if last:
+                o_hi = opool.tile([P, GL, C - TAIL], F32, name="o_hi", tag="o", align_bytes=64)
+                o_lo = opool.tile([P, GL, TAIL], F32, name="o_lo", tag="o", align_bytes=64)
+                parts = [(o_lo, 0, TAIL), (o_hi, TAIL, C)]
+            else:
+                o = opool.tile([P, GL, C], F32, name="o", tag="o", align_bytes=64)
+                parts = [(o, 0, C)]
             for l in range(LMAX, -1, -1):
                 d = 2 * l + 1
                 s0 = l * l
@@ -170,13 +176,14 @@ def tile_s2conv_pa_kernel(tc, x, psi, out):
                     nu = u1 - u0
                     src = acc[:, 0:nu * n].rearrange("p (u n) -> p u n", n=n)[:, :, off:off + GL * d]
                     src = src.rearrange("p u (g m) -> p g u m", m=d)
-                    dst = o[:, :, cl + u0 * d:cl + u1 * d].rearrange("p g (u m) -> p g u m", m=d)
+                    ca, cb = cl + u0 * d, cl + u1 * d
+                    ot, base = [(t, a) for t, a, b in parts if a <= ca and cb <= b][0]
+                    dst = ot[:, :, ca - base:cb - base].rearrange("p g (u m) -> p g u m", m=d)
                     if cl + u0 * d < VSPLIT:
                         nc.vector.tensor_scalar_mul(out=dst, in0=src, scalar1=SCALE)
                     else:
                         nc.scalar.activation(out=dst, in_=src, func=mybir.ActivationFunctionType.Copy, scale=SCALE)
                 if last and l == 5:
-                    lo_c = (cl + 7) // 8 * 8
-                    nc.sync.dma_start(out=out_v[:, GL * c:GL * c + GL, lo_c:done_to], in_=o[:, :, lo_c:done_to])
-                    done_to = lo_c
-            nc.sync.dma_start(out=out_v[:, GL * c:GL * c + GL, 0:done_to], in_=o[:, :, 0:done_to])
+                    nc.sync.dma_start(out=out_v[:, GL * c:GL * c + GL, TAIL:C], in_=o_hi[:])
+            ot, a, b = parts[0]
+            nc.sync.dma_start(out=out_v[:, GL * c:GL * c + GL, a:b], in_=ot[:])

@@ -18,6 +18,7 @@ GL = 16
 NCHUNK = 4
 SCALE = 1.0 / (512.0 ** 0.5)
 FLOPS = 2 * F * B * G * C
+RUNS = 4
 TAIL = 176
 VSPLIT = 176
 
@@ -76,13 +77,11 @@ def tile_s2conv_pa_kernel(tc, x, psi, out):
             state["next"] = k + 1
             kind, a, h = order[k]
             raw = rawp.tile([P, 16, 256], BF16, name="raw", tag="raw")
-            if kind == "p":
-                nc.sync.dma_start(out=raw[:], in_=psi_v[h][:, GL * a:GL * a + GL, :])
-            elif a == 48:
-                nc.sync.dma_start(out=raw[:, 0:8, :], in_=x_v[:, a:a + 8, :])
-                nc.sync.dma_start(out=raw[:, 8:16, :], in_=x_v[:, a + 8:a + 16, :])
-            else:
-                nc.sync.dma_start(out=raw[:], in_=x_v[:, a:a + 16, :])
+            for r in range(0, 16, RUNS):
+                if kind == "p":
+                    nc.sync.dma_start(out=raw[:, r:r + RUNS, :], in_=psi_v[h][:, GL * a + r:GL * a + r + RUNS, :])
+                else:
+                    nc.sync.dma_start(out=raw[:, r:r + RUNS, :], in_=x_v[:, a + r:a + r + RUNS, :])
             loaded[order[k]] = raw
 
         for k in range(4):
@@ -184,6 +183,8 @@ def tile_s2conv_pa_kernel(tc, x, psi, out):
                     else:
                         nc.scalar.activation(out=dst, in_=src, func=mybir.ActivationFunctionType.Copy, scale=SCALE)
                 if last and l == 5:
-                    nc.sync.dma_start(out=out_v[:, GL * c:GL * c + GL, TAIL:C], in_=o_hi[:])
+                    for r in range(0, GL, RUNS):
+                        nc.sync.dma_start(out=out_v[:, GL * c + r:GL * c + r + RUNS, TAIL:C], in_=o_hi[:, r:r + RUNS, :])
             ot, a, b = parts[0]
-            nc.sync.dma_start(out=out_v[:, GL * c:GL * c + GL, a:b], in_=ot[:])
+            for r in range(0, GL, RUNS):
+                nc.sync.dma_start(out=out_v[:, GL * c + r:GL * c + r + RUNS, a:b], in_=ot[:, r:r + RUNS, :])

@@ -18,7 +18,6 @@ GL = 16
 NCHUNK = 4
 SCALE = 1.0 / (512.0 ** 0.5)
 FLOPS = 2 * F * B * G * C
-RUNS = 4
 TAIL = 176
 VSPLIT = 176
 
@@ -77,11 +76,14 @@ def tile_s2conv_pa_kernel(tc, x, psi, out):
             state["next"] = k + 1
             kind, a, h = order[k]
             raw = rawp.tile([P, 16, 256], BF16, name="raw", tag="raw")
-            for r in range(0, 16, RUNS):
-                if kind == "p":
-                    nc.sync.dma_start(out=raw[:, r:r + RUNS, :], in_=psi_v[h][:, GL * a + r:GL * a + r + RUNS, :])
-                else:
-                    nc.sync.dma_start(out=raw[:, r:r + RUNS, :], in_=x_v[:, a + r:a + r + RUNS, :])
+            if kind == "p":
+                nc.sync.dma_start(out=raw[:], in_=psi_v[h][:, GL * a:GL * a + GL, :])
+            elif a == 48:
+                nc.sync.dma_start(out=raw[:, 0:8, :], in_=x_v[:, a:a + 8, :])
+                nc.sync.dma_start(out=raw[:, 8:12, :], in_=x_v[:, a + 8:a + 12, :])
+                nc.sync.dma_start(out=raw[:, 12:16, :], in_=x_v[:, a + 12:a + 16, :])
+            else:
+                nc.sync.dma_start(out=raw[:], in_=x_v[:, a:a + 16, :])
             loaded[order[k]] = raw
 
         for k in range(4):
@@ -117,7 +119,7 @@ def tile_s2conv_pa_kernel(tc, x, psi, out):
         for b0 in (0, 16, 32, 48):
             raw = loaded[("x", b0, 0)]
             if b0 == 48:
-                parts = (("v", 0, 4), ("s", 4, 4), ("v", 8, 4), ("s", 12, 4))
+                parts = (("v", 0, 4), ("s", 4, 4), ("s", 8, 4), ("v", 12, 4))
             else:
                 parts = (("v", 0, 12), ("s", 12, 4))
             for eng, a, n in parts:
@@ -140,7 +142,7 @@ def tile_s2conv_pa_kernel(tc, x, psi, out):
             pc, ps = pcs
             if c + 1 < NCHUNK:
                 pcs = prep_psi(c + 1)
-            last = c == NCHUNK - 1
+            last = c >= NCHUNK - 2
             if last:
                 o_hi = opool.tile([P, GL, C - TAIL], F32, name="o_hi", tag="o", align_bytes=64)
                 o_lo = opool.tile([P, GL, TAIL], F32, name="o_lo", tag="o", align_bytes=64)
@@ -183,8 +185,6 @@ def tile_s2conv_pa_kernel(tc, x, psi, out):
                     else:
                         nc.scalar.activation(out=dst, in_=src, func=mybir.ActivationFunctionType.Copy, scale=SCALE)
                 if last and l == 5:
-                    for r in range(0, GL, RUNS):
-                        nc.sync.dma_start(out=out_v[:, GL * c + r:GL * c + r + RUNS, TAIL:C], in_=o_hi[:, r:r + RUNS, :])
+                    nc.sync.dma_start(out=out_v[:, GL * c:GL * c + GL, TAIL:C], in_=o_hi[:])
             ot, a, b = parts[0]
-            for r in range(0, GL, RUNS):
-                nc.sync.dma_start(out=out_v[:, GL * c + r:GL * c + r + RUNS, a:b], in_=ot[:, r:r + RUNS, :])
+            nc.sync.dma_start(out=out_v[:, GL * c:GL * c + GL, a:b], in_=ot[:])

@@ -53,6 +53,7 @@ def tile_s2conv_pa_kernel(tc, x, psi, out):
         gpool = ctx.enter_context(tc.tile_pool(name="gpool", bufs=2))
         opool = ctx.enter_context(tc.tile_pool(name="opool", bufs=3))
         psum = ctx.enter_context(tc.psum_pool(name="psum", bufs=8))
+        ctx.enter_context(tc.manual_schedule())
 
         xc = keep.tile([P, 64 + 128 * S2], U32, name="xc", align_bytes=64)
         xs = keep.tile([P, 64 + 128 * S2], U8, name="xs", align_bytes=64)

@@ -50,7 +50,8 @@ def tile_s2conv_pa_kernel(tc, x, psi, out):
     with ExitStack() as ctx:
         keep = ctx.enter_context(tc.tile_pool(name="keep", bufs=1))
         rawp = ctx.enter_context(tc.tile_pool(name="rawp", bufs=4))
-        gpool = ctx.enter_context(tc.tile_pool(name="gpool", bufs=2))
+        cpool = ctx.enter_context(tc.tile_pool(name="cpool", bufs=2))
+        gpool = ctx.enter_context(tc.tile_pool(name="gpool", bufs=4))
         opool = ctx.enter_context(tc.tile_pool(name="opool", bufs=3))
         psum = ctx.enter_context(tc.psum_pool(name="psum", bufs=8))
         ctx.enter_context(tc.manual_schedule())
@@ -64,11 +65,11 @@ def tile_s2conv_pa_kernel(tc, x, psi, out):
         nc.vector.memset(xsi[:, 0:2048].rearrange("p (k w) -> p k w", w=32)[:, :, 0:16], 0)
         nc.vector.memset(xsi[:, 2048:2064], 0)
 
-        order = [("p", 0, 0), ("p", 0, 1), ("x", 0, 0), ("x", 16, 0), ("x", 32, 0), ("x", 48, 0)]
-        for c in range(1, NCHUNK):
+        order = [("x", 0, 0), ("x", 16, 0), ("x", 32, 0), ("x", 48, 0)]
+        for c in range(NCHUNK):
             order.extend([("p", c, 0), ("p", c, 1)])
         loaded = {}
-        state = {"next": 0}
+        state = {"next": 0, "qx": 0}
 
         def load_next():
             k = state["next"]
@@ -90,39 +91,13 @@ def tile_s2conv_pa_kernel(tc, x, psi, out):
         for k in range(4):
             load_next()
 
-        def prep_psi(c):
-            pc = gpool.tile([P, 2, 1024], U32, name="pc", tag="pc", align_bytes=64)
-            ps = gpool.tile([P, 2, 1024], U8, name="ps", tag="ps", align_bytes=64)
-            for h in range(2):
-                raw = loaded[("p", c, h)]
-                gp = gpool.tile([P, 4, 256, 4], BF16, name="gp", tag="gp", align_bytes=64)
-                rv = raw[:].rearrange("p gl (t s) -> p gl t s", t=4)
-                for j in range(4):
-                    for l, off in ((7 - j, 0), (j, GL * (15 - 2 * j))):
-                        d = 2 * l + 1
-                        s0 = l * l
-                        nc.vector.tensor_copy(
-                            out=gp[:, j, off:off + GL * d, :].rearrange("p (gl m) t -> p gl m t", m=d),
-                            in_=rv[:, :, :, s0:s0 + d].rearrange("p gl t m -> p gl m t"),
-                        )
-                load_next()
-                for q in range(2):
-                    nc.vector.quantize_mx(
-                        out=pc[:, h, 512 * q:512 * q + 512].bitcast(FP8X4),
-                        scales=ps[:, h, 512 * q:512 * q + 512],
-                        in_=gp[:, 2 * q:2 * q + 2].rearrange("p j w t -> p (j w t)"),
-                    )
-            return pc, ps
-
-        pcs = prep_psi(0)
-
         xg = opool.tile([P, S2, B, 4], BF16, name="xg", tag="o", align_bytes=64)
         for b0 in (0, 16, 32, 48):
             raw = loaded[("x", b0, 0)]
             if b0 == 48:
                 parts = (("v", 0, 4), ("s", 4, 4), ("s", 8, 4), ("v", 12, 4))
             else:
-                parts = (("v", 0, 12), ("s", 12, 4))
+                parts = (("v", 0, 10), ("s", 10, 6))
             for eng, a, n in parts:
                 src = raw[:, a:a + n, :].rearrange("p b (t s) -> p b s t", t=4)
                 dst = xg[:, :, b0 + a:b0 + a + n, :].rearrange("p s b t -> p b s t")
@@ -131,19 +106,86 @@ def tile_s2conv_pa_kernel(tc, x, psi, out):
                 else:
                     nc.scalar.copy(out=dst, in_=src)
             load_next()
-        for s in reversed(range(S2)):
-            lo = 128 * s + 64
+
+        s_order = []
+        for l in range(LMAX, -1, -1):
+            s_order.extend(range(l * l, (l + 1) * (l + 1)))
+
+        def qx(n):
+            for s in s_order[state["qx"]:state["qx"] + n]:
+                lo = 128 * s + 64
+                nc.vector.quantize_mx(
+                    out=xc[:, lo:lo + 64].bitcast(FP8X4),
+                    scales=xs[:, lo:lo + 64],
+                    in_=xg[:, s].rearrange("p b t -> p (b t)"),
+                )
+            state["qx"] = state["qx"] + n
+
+        def code_tiles():
+            pc = cpool.tile([P, 2, 1024], U32, name="pc", tag="pc", align_bytes=64)
+            ps = cpool.tile([P, 2, 1024], U8, name="ps", tag="ps", align_bytes=64)
+            return pc, ps
+
+        def copy_slot(c, h, j):
+            raw = loaded[("p", c, h)]
+            gp = gpool.tile([P, 256, 4], BF16, name="gp", tag="gp", align_bytes=64)
+            rv = raw[:].rearrange("p gl (t s) -> p gl t s", t=4)
+            for l, off in ((7 - j, 0), (j, GL * (15 - 2 * j))):
+                d = 2 * l + 1
+                s0 = l * l
+                nc.vector.tensor_copy(
+                    out=gp[:, off:off + GL * d, :].rearrange("p (gl m) t -> p gl m t", m=d),
+                    in_=rv[:, :, :, s0:s0 + d].rearrange("p gl t m -> p gl m t"),
+                )
+            return gp
+
+        def quant_slot(pcs, h, j, gp):
+            pc, ps = pcs
             nc.vector.quantize_mx(
-                out=xc[:, lo:lo + 64].bitcast(FP8X4),
-                scales=xs[:, lo:lo + 64],
-                in_=xg[:, s].rearrange("p b t -> p (b t)"),
+                out=pc[:, h, 256 * j:256 * j + 256].bitcast(FP8X4),
+                scales=ps[:, h, 256 * j:256 * j + 256],
+                in_=gp[:].rearrange("p w t -> p (w t)"),
             )
+
+        pcs = code_tiles()
+        qx(15)
+        ga = copy_slot(0, 0, 0)
+        qx(4)
+        quant_slot(pcs, 0, 0, ga)
+        gb = copy_slot(0, 1, 0)
+        qx(4)
+        quant_slot(pcs, 1, 0, gb)
+        for j, n in ((1, 5), (2, 11), (3, 9)):
+            ga = copy_slot(0, 0, j)
+            gb = copy_slot(0, 1, j)
+            qx(n)
+            quant_slot(pcs, 0, j, ga)
+            quant_slot(pcs, 1, j, gb)
+        load_next()
+        load_next()
+        qx(16)
+
+        def prep_psi(c):
+            new = code_tiles()
+            held = []
+            for j in range(4):
+                ga = copy_slot(c, 0, j)
+                gb = copy_slot(c, 1, j)
+                for h, jj, g in held:
+                    quant_slot(new, h, jj, g)
+                held = [(0, j, ga), (1, j, gb)]
+            load_next()
+            load_next()
+            for h, jj, g in held:
+                quant_slot(new, h, jj, g)
+            return new
 
         for c in range(NCHUNK):
             pc, ps = pcs
             if c + 1 < NCHUNK:
                 pcs = prep_psi(c + 1)
             last = c >= NCHUNK - 2
+            vsplit = 0 if c == 0 else VSPLIT
             if last:
                 o_hi = opool.tile([P, GL, C - TAIL], F32, name="o_hi", tag="o", align_bytes=64)
                 o_lo = opool.tile([P, GL, TAIL], F32, name="o_lo", tag="o", align_bytes=64)
@@ -181,7 +223,7 @@ def tile_s2conv_pa_kernel(tc, x, psi, out):
                     ca, cb = cl + u0 * d, cl + u1 * d
                     ot, base = [(t, a) for t, a, b in parts if a <= ca and cb <= b][0]
                     dst = ot[:, :, ca - base:cb - base].rearrange("p g (u m) -> p g u m", m=d)
-                    if cl + u0 * d < VSPLIT:
+                    if cl + u0 * d < vsplit:
                         nc.vector.tensor_scalar_mul(out=dst, in0=src, scalar1=SCALE)
                     else:
                         nc.scalar.activation(out=dst, in_=src, func=mybir.ActivationFunctionType.Copy, scale=SCALE)

@@ -18,8 +18,9 @@ GL = 16
 NCHUNK = 4
 SCALE = 1.0 / (512.0 ** 0.5)
 FLOPS = 2 * F * B * G * C
-TAIL = 176
 VSPLIT = 176
+CUTS = ((), (), (176,), (176, 416))
+ALL_CUTS = (176, 416)
 
 
 def c_of(l):
@@ -31,7 +32,7 @@ def u_groups(l):
     per = 2 if l >= 4 else 4
     cuts = [0, d]
     for u in range(1, d):
-        if c_of(l) + u * d == VSPLIT:
+        if c_of(l) + u * d in ALL_CUTS:
             cuts.append(u)
     cuts = sorted(cuts)
     groups = []
@@ -107,9 +108,7 @@ def tile_s2conv_pa_kernel(tc, x, psi, out):
                     nc.scalar.copy(out=dst, in_=src)
             load_next()
 
-        s_order = []
-        for l in range(LMAX, -1, -1):
-            s_order.extend(range(l * l, (l + 1) * (l + 1)))
+        s_order = list(reversed(range(S2)))
 
         def qx(n):
             for s in s_order[state["qx"]:state["qx"] + n]:
@@ -184,15 +183,10 @@ def tile_s2conv_pa_kernel(tc, x, psi, out):
             pc, ps = pcs
             if c + 1 < NCHUNK:
                 pcs = prep_psi(c + 1)
-            last = c >= NCHUNK - 2
             vsplit = 0 if c == 0 else VSPLIT
-            if last:
-                o_hi = opool.tile([P, GL, C - TAIL], F32, name="o_hi", tag="o", align_bytes=64)
-                o_lo = opool.tile([P, GL, TAIL], F32, name="o_lo", tag="o", align_bytes=64)
-                parts = [(o_lo, 0, TAIL), (o_hi, TAIL, C)]
-            else:
-                o = opool.tile([P, GL, C], F32, name="o", tag="o", align_bytes=64)
-                parts = [(o, 0, C)]
+            o = opool.tile([P, GL * C], F32, name="o", tag="o", align_bytes=64)
+            bounds = [0] + list(CUTS[c]) + [C]
+            segs = list(zip(bounds[:-1], bounds[1:]))
             for l in range(LMAX, -1, -1):
                 d = 2 * l + 1
                 s0 = l * l
@@ -202,7 +196,7 @@ def tile_s2conv_pa_kernel(tc, x, psi, out):
                 else:
                     j, n, w0, off = l, 128, 128, GL * (15 - 2 * l) - 128
                 w0 = w0 + 256 * j
-                for u0, u1 in u_groups(l):
+                for u0, u1 in reversed(u_groups(l)):
                     acc = psum.tile([P, 512], F32, name="acc", tag="acc")
                     for i, u in enumerate(range(u0, u1)):
                         s = s0 + u
@@ -221,13 +215,12 @@ def tile_s2conv_pa_kernel(tc, x, psi, out):
                     src = acc[:, 0:nu * n].rearrange("p (u n) -> p u n", n=n)[:, :, off:off + GL * d]
                     src = src.rearrange("p u (g m) -> p g u m", m=d)
                     ca, cb = cl + u0 * d, cl + u1 * d
-                    ot, base = [(t, a) for t, a, b in parts if a <= ca and cb <= b][0]
-                    dst = ot[:, :, ca - base:cb - base].rearrange("p g (u m) -> p g u m", m=d)
-                    if cl + u0 * d < vsplit:
+                    a, b = [(a, b) for a, b in segs if a <= ca and cb <= b][0]
+                    seg = o[:, GL * a:GL * b].rearrange("p (g k) -> p g k", g=GL)
+                    dst = seg[:, :, ca - a:cb - a].rearrange("p g (u m) -> p g u m", m=d)
+                    if ca < vsplit:
                         nc.vector.tensor_scalar_mul(out=dst, in0=src, scalar1=SCALE)
                     else:
                         nc.scalar.activation(out=dst, in_=src, func=mybir.ActivationFunctionType.Copy, scale=SCALE)
-                if last and l == 5:
-                    nc.sync.dma_start(out=out_v[:, GL * c:GL * c + GL, TAIL:C], in_=o_hi[:])
-            ot, a, b = parts[0]
-            nc.sync.dma_start(out=out_v[:, GL * c:GL * c + GL, a:b], in_=ot[:])
+                    if ca == a:
+                        nc.sync.dma_start(out=out_v[:, GL * c:GL * c + GL, a:b], in_=seg)

@@ -66,33 +66,32 @@ def tile_s2conv_pa_kernel(tc, x, psi, out):
         nc.vector.memset(xsi[:, 0:2048].rearrange("p (k w) -> p k w", w=32)[:, :, 0:16], 0)
         nc.vector.memset(xsi[:, 2048:2064], 0)
 
-        order = [("x", 0, 0), ("x", 16, 0), ("x", 32, 0), ("x", 48, 0)]
-        for c in range(NCHUNK):
-            order.extend([("p", c, 0), ("p", c, 1)])
         loaded = {}
-        state = {"next": 0, "qx": 0}
+        state = {"qx": 0}
 
-        def load_next():
-            k = state["next"]
-            if k >= len(order):
-                return
-            state["next"] = k + 1
-            kind, a, h = order[k]
+        def load_x(a):
             raw = rawp.tile([P, 16, 256], BF16, name="raw", tag="raw")
-            if kind == "p":
-                nc.sync.dma_start(out=raw[:], in_=psi_v[h][:, GL * a:GL * a + GL, :])
-            elif a == 48:
+            if a == 48:
                 nc.sync.dma_start(out=raw[:, 0:8, :], in_=x_v[:, a:a + 8, :])
                 nc.sync.dma_start(out=raw[:, 8:12, :], in_=x_v[:, a + 8:a + 12, :])
                 nc.sync.dma_start(out=raw[:, 12:16, :], in_=x_v[:, a + 12:a + 16, :])
             else:
                 nc.sync.dma_start(out=raw[:], in_=x_v[:, a:a + 16, :])
-            loaded[order[k]] = raw
+            loaded[("x", a, 0)] = raw[:]
 
-        for k in range(4):
-            load_next()
+        def load_psi(c, h, dst):
+            nc.sync.dma_start(out=dst, in_=psi_v[h][:, GL * c:GL * c + GL, :])
+            loaded[("p", c, h)] = dst
+
+        def load_psi_small(c, h):
+            raw = rawp.tile([P, 16, 256], BF16, name="raw", tag="raw")
+            load_psi(c, h, raw[:])
+
+        for b0 in (0, 16, 32, 48):
+            load_x(b0)
 
         xg = opool.tile([P, S2, B, 4], BF16, name="xg", tag="o", align_bytes=64)
+        rawbig = opool.tile([P, 4, 16, 256], BF16, name="rawbig", tag="o", align_bytes=64)
         for b0 in (0, 16, 32, 48):
             raw = loaded[("x", b0, 0)]
             if b0 == 48:
@@ -106,7 +105,16 @@ def tile_s2conv_pa_kernel(tc, x, psi, out):
                     nc.vector.tensor_copy(out=dst, in_=src)
                 else:
                     nc.scalar.copy(out=dst, in_=src)
-            load_next()
+            if b0 == 0:
+                load_psi_small(0, 0)
+            elif b0 == 16:
+                load_psi_small(0, 1)
+                for i, (c, h) in enumerate(((1, 0), (1, 1), (2, 0), (2, 1))):
+                    load_psi(c, h, rawbig[:, i])
+            elif b0 == 32:
+                load_psi_small(3, 0)
+            else:
+                load_psi_small(3, 1)
 
         s_order = list(reversed(range(S2)))
 
@@ -128,7 +136,7 @@ def tile_s2conv_pa_kernel(tc, x, psi, out):
         def copy_slot(c, h, j):
             raw = loaded[("p", c, h)]
             gp = gpool.tile([P, 256, 4], BF16, name="gp", tag="gp", align_bytes=64)
-            rv = raw[:].rearrange("p gl (t s) -> p gl t s", t=4)
+            rv = raw.rearrange("p gl (t s) -> p gl t s", t=4)
             for l, off in ((7 - j, 0), (j, GL * (15 - 2 * j))):
                 d = 2 * l + 1
                 s0 = l * l
@@ -160,8 +168,6 @@ def tile_s2conv_pa_kernel(tc, x, psi, out):
             qx(n)
             quant_slot(pcs, 0, j, ga)
             quant_slot(pcs, 1, j, gb)
-        load_next()
-        load_next()
         qx(16)
 
         def prep_psi(c):
@@ -173,8 +179,6 @@ def tile_s2conv_pa_kernel(tc, x, psi, out):
                 for h, jj, g in held:
                     quant_slot(new, h, jj, g)
                 held = [(0, j, ga), (1, j, gb)]
-            load_next()
-            load_next()
             for h, jj, g in held:
                 quant_slot(new, h, jj, g)
             return new

@@ -18,7 +18,7 @@ GL = 16
 NCHUNK = 4
 SCALE = 1.0 / (512.0 ** 0.5)
 FLOPS = 2 * F * B * G * C
-VSPLIT = 176
+VTURN = (0, 4, 4, 2)
 CUTS = ((), (), (176,), (176, 416))
 ALL_CUTS = (176, 416)
 
@@ -170,37 +170,48 @@ def tile_s2conv_pa_kernel(tc, x, psi, out):
             quant_slot(pcs, 1, j, gb)
         qx(16)
 
-        def prep_psi(c):
-            new = code_tiles()
-            held = []
+        def prep_steps(c, new):
+            steps = []
             for j in range(4):
-                ga = copy_slot(c, 0, j)
-                gb = copy_slot(c, 1, j)
-                for h, jj, g in held:
-                    quant_slot(new, h, jj, g)
-                held = [(0, j, ga), (1, j, gb)]
-            for h, jj, g in held:
-                quant_slot(new, h, jj, g)
-            return new
+                steps.extend([("copy", 0, j), ("copy", 1, j), ("quant", 0, j), ("quant", 1, j)])
+            return steps
+
+        staged = {}
+
+        def run_step(c, new, step):
+            kind, h, j = step
+            if kind == "copy":
+                staged[(h, j)] = copy_slot(c, h, j)
+            else:
+                quant_slot(new, h, j, staged[(h, j)])
 
         for c in range(NCHUNK):
             pc, ps = pcs
+            steps = []
             if c + 1 < NCHUNK:
-                pcs = prep_psi(c + 1)
-            vsplit = 0 if c == 0 else VSPLIT
+                pcs = code_tiles()
+                steps = prep_steps(c + 1, pcs)
+            done = 0
+            groups = []
+            for l in range(LMAX, -1, -1):
+                groups.extend([(l, u0, u1) for u0, u1 in reversed(u_groups(l))])
             o = opool.tile([P, GL * C], F32, name="o", tag="o", align_bytes=64)
             bounds = [0] + list(CUTS[c]) + [C]
             segs = list(zip(bounds[:-1], bounds[1:]))
-            for l in range(LMAX, -1, -1):
-                d = 2 * l + 1
-                s0 = l * l
-                cl = c_of(l)
-                if l >= 4:
-                    j, n, w0, off = 7 - l, 256, 0, 0
-                else:
-                    j, n, w0, off = l, 128, 128, GL * (15 - 2 * l) - 128
-                w0 = w0 + 256 * j
-                for u0, u1 in reversed(u_groups(l)):
+            for gi, (l, u0, u1) in enumerate(groups):
+                if True:
+                    want = min(len(steps), (len(steps) * (gi + 1) + 23) // 24)
+                    while done < want:
+                        run_step(c + 1, pcs, steps[done])
+                        done = done + 1
+                    d = 2 * l + 1
+                    s0 = l * l
+                    cl = c_of(l)
+                    if l >= 4:
+                        j, n, w0, off = 7 - l, 256, 0, 0
+                    else:
+                        j, n, w0, off = l, 128, 128, GL * (15 - 2 * l) - 128
+                    w0 = w0 + 256 * j
                     acc = psum.tile([P, 512], F32, name="acc", tag="acc")
                     for i, u in enumerate(range(u0, u1)):
                         s = s0 + u
@@ -222,7 +233,7 @@ def tile_s2conv_pa_kernel(tc, x, psi, out):
                     a, b = [(a, b) for a, b in segs if a <= ca and cb <= b][0]
                     seg = o[:, GL * a:GL * b].rearrange("p (g k) -> p g k", g=GL)
                     dst = seg[:, :, ca - a:cb - a].rearrange("p g (u m) -> p g u m", m=d)
-                    if ca < vsplit:
+                    if VTURN[c] > 0 and gi % VTURN[c] == VTURN[c] - 1:
                         nc.vector.tensor_scalar_mul(out=dst, in0=src, scalar1=SCALE)
                     else:
                         nc.scalar.activation(out=dst, in_=src, func=mybir.ActivationFunctionType.Copy, scale=SCALE)

@@ -19,7 +19,7 @@ NCHUNK = 4
 SCALE = 1.0 / (512.0 ** 0.5)
 FLOPS = 2 * F * B * G * C
 VTURN = (0, 4, 4, 2)
-CUTS = ((), (), (176,), (176, 416))
+CUTS = ((176, 416), (176, 416), (176, 416), (176, 416))
 ALL_CUTS = (176, 416)
 
 

@@ -19,8 +19,8 @@ NCHUNK = 4
 SCALE = 1.0 / (512.0 ** 0.5)
 FLOPS = 2 * F * B * G * C
 VTURN = (0, 4, 4, 2)
-CUTS = ((176, 416), (176, 416), (176, 416), (176, 416))
-ALL_CUTS = (176, 416)
+CUTS = ((312,), (176, 416), (176, 416), (176, 416))
+ALL_CUTS = (176, 312, 416)
 
 
 def c_of(l):

@@ -1,8 +1,6 @@
 from contextlib import ExitStack
 
-import concourse.bass as bass
 import concourse.mybir as mybir
-import concourse.tile as tile
 
 FP8X4 = mybir.dt.float8_e4m3fn_x4
 BF16 = mybir.dt.bfloat16
@@ -14,228 +12,212 @@ I32 = mybir.dt.int32
 P = 128
 B, F, G, S2, LMAX = 64, 512, 128, 64, 7
 C = 680
-GL = 16
-NCHUNK = 4
+NQ = 64
+RING = 32
+STEP = 8
+NSTAGE = NQ // STEP
 SCALE = 1.0 / (512.0 ** 0.5)
 FLOPS = 2 * F * B * G * C
-VTURN = (0, 4, 4, 2)
-CUTS = ((312,), (176, 416), (176, 416), (176, 416))
-ALL_CUTS = (176, 312, 416)
+XG0 = RING * C - S2 * B * 2
 
 
 def c_of(l):
     return sum((2 * k + 1) ** 2 for k in range(l))
 
 
-def u_groups(l):
+def q_windows(l):
     d = 2 * l + 1
-    per = 2 if l >= 4 else 4
-    cuts = [0, d]
-    for u in range(1, d):
-        if c_of(l) + u * d in ALL_CUTS:
-            cuts.append(u)
-    cuts = sorted(cuts)
-    groups = []
-    for a, b in zip(cuts[:-1], cuts[1:]):
-        for u0 in range(a, b, per):
-            groups.append((u0, min(u0 + per, b)))
-    return groups
+    n = min(24, 128 // d)
+    out = []
+    q = 0
+    while q < NQ:
+        rem = NQ - q
+        if rem > 2 * n and rem <= min(24, 256 // d):
+            out.append((q, NQ, 256))
+            q = NQ
+        else:
+            out.append((q, min(q + n, NQ), 128))
+            q = min(q + n, NQ)
+    return out
 
 
 def tile_s2conv_pa_kernel(tc, x, psi, out):
     nc = tc.nc
     x_v = x.rearrange("b (p t) s -> p b (t s)", t=4)
-    psi_v = psi.rearrange("(gl h) (p t) s -> h p gl (t s)", h=2, t=4)
-    out_v = out.flatten_outer_dims().rearrange("(gl p) c -> p gl c", p=P)
+    psi_v = psi.rearrange("g (p t) s -> p g (t s)", t=4)
+    out_v = out.flatten_outer_dims().rearrange("(q p) c -> p q c", p=P)
 
     with ExitStack() as ctx:
         keep = ctx.enter_context(tc.tile_pool(name="keep", bufs=1))
-        rawp = ctx.enter_context(tc.tile_pool(name="rawp", bufs=4))
-        cpool = ctx.enter_context(tc.tile_pool(name="cpool", bufs=2))
-        gpool = ctx.enter_context(tc.tile_pool(name="gpool", bufs=4))
-        opool = ctx.enter_context(tc.tile_pool(name="opool", bufs=3))
+        cpool = ctx.enter_context(tc.tile_pool(name="cpool", bufs=14))
         psum = ctx.enter_context(tc.psum_pool(name="psum", bufs=8))
         ctx.enter_context(tc.manual_schedule())
 
         xc = keep.tile([P, 64 + 128 * S2], U32, name="xc", align_bytes=64)
         xs = keep.tile([P, 64 + 128 * S2], U8, name="xs", align_bytes=64)
+        raw = keep.tile([P, G, 256], BF16, name="raw", align_bytes=64)
+        ring = keep.tile([P, RING * C], F32, name="ring", align_bytes=64)
+        gps = []
+        for i in range(4):
+            gp = keep.tile([P, 2, 128, 4], BF16, name="gp%d" % i, align_bytes=64)
+            gps.append(gp)
+        gpw = keep.tile([P, 2, 256, 4], BF16, name="gpw", align_bytes=64)
+        pcw = keep.tile([P, 2, 256], U32, name="pcw", align_bytes=64)
+        psw = keep.tile([P, 2, 256], U8, name="psw", align_bytes=64)
+
         xci = xc[:].bitcast(I32)
         xsi = xs[:].bitcast(I32)
         nc.vector.memset(xci[:, 0:8192].rearrange("p (k w) -> p k w", w=128)[:, :, 0:64], 0)
         nc.vector.memset(xci[:, 8192:8256], 0)
         nc.vector.memset(xsi[:, 0:2048].rearrange("p (k w) -> p k w", w=32)[:, :, 0:16], 0)
         nc.vector.memset(xsi[:, 2048:2064], 0)
+        for gp in gps:
+            nc.gpsimd.memset(gp[:], 0.0)
+        nc.gpsimd.memset(gpw[:], 0.0)
 
-        loaded = {}
-        state = {"qx": 0}
-
-        def load_x(a):
-            raw = rawp.tile([P, 16, 256], BF16, name="raw", tag="raw")
-            if a == 48:
-                nc.sync.dma_start(out=raw[:, 0:8, :], in_=x_v[:, a:a + 8, :])
-                nc.sync.dma_start(out=raw[:, 8:12, :], in_=x_v[:, a + 8:a + 12, :])
-                nc.sync.dma_start(out=raw[:, 12:16, :], in_=x_v[:, a + 12:a + 16, :])
-            else:
-                nc.sync.dma_start(out=raw[:], in_=x_v[:, a:a + 16, :])
-            loaded[("x", a, 0)] = raw[:]
-
-        def load_psi(c, h, dst):
-            nc.sync.dma_start(out=dst, in_=psi_v[h][:, GL * c:GL * c + GL, :])
-            loaded[("p", c, h)] = dst
-
-        def load_psi_small(c, h):
-            raw = rawp.tile([P, 16, 256], BF16, name="raw", tag="raw")
-            load_psi(c, h, raw[:])
-
+        xg = ring[:, XG0:RING * C].bitcast(BF16).rearrange("p (s b t) -> p s b t", s=S2, b=B)
+        xraw = raw[:, 64:128, :]
+        for b0, n in ((0, 16), (16, 16), (32, 16), (48, 8), (56, 4), (60, 4)):
+            nc.sync.dma_start(out=xraw[:, b0:b0 + n, :], in_=x_v[:, b0:b0 + n, :])
+        for g0 in range(0, 64, 16):
+            nc.sync.dma_start(out=raw[:, g0:g0 + 16, :], in_=psi_v[:, g0:g0 + 16, :])
         for b0 in (0, 16, 32, 48):
-            load_x(b0)
-
-        xg = opool.tile([P, S2, B, 4], BF16, name="xg", tag="o", align_bytes=64)
-        rawbig = opool.tile([P, 4, 16, 256], BF16, name="rawbig", tag="o", align_bytes=64)
-        for b0 in (0, 16, 32, 48):
-            raw = loaded[("x", b0, 0)]
             if b0 == 48:
                 parts = (("v", 0, 4), ("s", 4, 4), ("s", 8, 4), ("v", 12, 4))
             else:
                 parts = (("v", 0, 10), ("s", 10, 6))
             for eng, a, n in parts:
-                src = raw[:, a:a + n, :].rearrange("p b (t s) -> p b s t", t=4)
-                dst = xg[:, :, b0 + a:b0 + a + n, :].rearrange("p s b t -> p b s t")
+                lo = b0 + a
+                src = xraw[:, lo:lo + n, :].rearrange("p b (t s) -> p b s t", t=4)
+                dst = xg[:, :, lo:lo + n, :].rearrange("p s b t -> p b s t")
                 if eng == "v":
                     nc.vector.tensor_copy(out=dst, in_=src)
                 else:
                     nc.scalar.copy(out=dst, in_=src)
-            if b0 == 0:
-                load_psi_small(0, 0)
-            elif b0 == 16:
-                load_psi_small(0, 1)
-                for i, (c, h) in enumerate(((1, 0), (1, 1), (2, 0), (2, 1))):
-                    load_psi(c, h, rawbig[:, i])
-            elif b0 == 32:
-                load_psi_small(3, 0)
-            else:
-                load_psi_small(3, 1)
+        for g0 in range(64, 128, 16):
+            nc.sync.dma_start(out=raw[:, g0:g0 + 16, :], in_=psi_v[:, g0:g0 + 16, :])
 
-        s_order = list(reversed(range(S2)))
-
-        def qx(n):
-            for s in s_order[state["qx"]:state["qx"] + n]:
+        def qx(s0, s1):
+            for s in range(s0, s1):
                 lo = 128 * s + 64
                 nc.vector.quantize_mx(
                     out=xc[:, lo:lo + 64].bitcast(FP8X4),
                     scales=xs[:, lo:lo + 64],
                     in_=xg[:, s].rearrange("p b t -> p (b t)"),
                 )
-            state["qx"] = state["qx"] + n
 
-        def code_tiles():
-            pc = cpool.tile([P, 2, 1024], U32, name="pc", tag="pc", align_bytes=64)
-            ps = cpool.tile([P, 2, 1024], U8, name="ps", tag="ps", align_bytes=64)
-            return pc, ps
+        todo = [q_windows(l) for l in range(LMAX + 1)]
+        wins = []
+        slots = []
+        for st in range(NSTAGE):
+            for l in range(LMAX, -1, -1):
+                while len(todo[l]) > 0 and todo[l][0][0] < STEP * (st + 1):
+                    q0, q1, n = todo[l].pop(0)
+                    off = 0
+                    if l == 0:
+                        off = 3 * (q1 - q0)
+                        slots[-1]["parts"].append((l, q0, q1, off))
+                    else:
+                        slots.append({"parts": [(l, q0, q1, off)], "n": n, "k": len(slots)})
+                    wins.append((st, l, q0, q1, n, off, len(slots) - 1))
 
-        def copy_slot(c, h, j):
-            raw = loaded[("p", c, h)]
-            gp = gpool.tile([P, 256, 4], BF16, name="gp", tag="gp", align_bytes=64)
-            rv = raw.rearrange("p gl (t s) -> p gl t s", t=4)
-            for l, off in ((7 - j, 0), (j, GL * (15 - 2 * j))):
+        rawv = raw[:].rearrange("p (q h) (t s) -> p h q s t", h=2, t=4)
+
+        def copy_slot(k):
+            slot = slots[k]
+            gp = gpw if slot["n"] == 256 else gps[k % len(gps)]
+            slot["gp"] = gp
+            for l, q0, q1, off in slot["parts"]:
                 d = 2 * l + 1
                 s0 = l * l
-                nc.vector.tensor_copy(
-                    out=gp[:, off:off + GL * d, :].rearrange("p (gl m) t -> p gl m t", m=d),
-                    in_=rv[:, :, :, s0:s0 + d].rearrange("p gl t m -> p gl m t"),
-                )
-            return gp
+                dst = gp[:, :, off:off + (q1 - q0) * d, :].rearrange("p h (q m) t -> p h q m t", m=d)
+                nc.vector.tensor_copy(out=dst, in_=rawv[:, :, q0:q1, s0:s0 + d, :])
 
-        def quant_slot(pcs, h, j, gp):
-            pc, ps = pcs
+        def quant_slot(k):
+            slot = slots[k]
+            n = slot["n"]
+            if n == 256:
+                pc, ps = pcw, psw
+            else:
+                pc = cpool.tile([P, 2, 128], U32, name="pc", tag="pc", align_bytes=64)
+                ps = cpool.tile([P, 2, 128], U8, name="ps", tag="ps", align_bytes=64)
+            slot["codes"] = (pc, ps)
             nc.vector.quantize_mx(
-                out=pc[:, h, 256 * j:256 * j + 256].bitcast(FP8X4),
-                scales=ps[:, h, 256 * j:256 * j + 256],
-                in_=gp[:].rearrange("p w t -> p (w t)"),
+                out=pc[:].rearrange("p h w -> p (h w)").bitcast(FP8X4),
+                scales=ps[:].rearrange("p h w -> p (h w)"),
+                in_=slot["gp"][:].rearrange("p h w t -> p (h w t)"),
             )
 
-        pcs = code_tiles()
-        qx(15)
-        ga = copy_slot(0, 0, 0)
-        qx(4)
-        quant_slot(pcs, 0, 0, ga)
-        gb = copy_slot(0, 1, 0)
-        qx(4)
-        quant_slot(pcs, 1, 0, gb)
-        for j, n in ((1, 5), (2, 11), (3, 9)):
-            ga = copy_slot(0, 0, j)
-            gb = copy_slot(0, 1, j)
-            qx(n)
-            quant_slot(pcs, 0, j, ga)
-            quant_slot(pcs, 1, j, gb)
-        qx(16)
+        copied = 0
+        quanted = 0
+        xdone = []
 
-        def prep_steps(c, new):
-            steps = []
-            for j in range(4):
-                steps.extend([("copy", 0, j), ("copy", 1, j), ("quant", 0, j), ("quant", 1, j)])
-            return steps
+        def prep_copy(k):
+            if k < len(slots):
+                copy_slot(k)
 
-        staged = {}
+        def prep_quant(k):
+            if k < len(slots):
+                for l, q0, q1, off in slots[k]["parts"]:
+                    if l not in xdone:
+                        qx(l * l, (l + 1) ** 2)
+                        xdone.append(l)
+                quant_slot(k)
 
-        def run_step(c, new, step):
-            kind, h, j = step
-            if kind == "copy":
-                staged[(h, j)] = copy_slot(c, h, j)
-            else:
-                quant_slot(new, h, j, staged[(h, j)])
+        qx(49, 60)
+        copy_slot(0)
+        qx(60, 64)
+        xdone.append(7)
+        quant_slot(0)
+        copy_slot(1)
+        prep_quant(1)
+        copy_slot(2)
+        ready = 1
 
-        for c in range(NCHUNK):
-            pc, ps = pcs
-            steps = []
-            if c + 1 < NCHUNK:
-                pcs = code_tiles()
-                steps = prep_steps(c + 1, pcs)
-            done = 0
-            groups = []
-            for l in range(LMAX, -1, -1):
-                groups.extend([(l, u0, u1) for u0, u1 in reversed(u_groups(l))])
-            o = opool.tile([P, GL * C], F32, name="o", tag="o", align_bytes=64)
-            bounds = [0] + list(CUTS[c]) + [C]
-            segs = list(zip(bounds[:-1], bounds[1:]))
-            for gi, (l, u0, u1) in enumerate(groups):
-                if True:
-                    want = min(len(steps), (len(steps) * (gi + 1) + 23) // 24)
-                    while done < want:
-                        run_step(c + 1, pcs, steps[done])
-                        done = done + 1
-                    d = 2 * l + 1
-                    s0 = l * l
-                    cl = c_of(l)
-                    if l >= 4:
-                        j, n, w0, off = 7 - l, 256, 0, 0
-                    else:
-                        j, n, w0, off = l, 128, 128, GL * (15 - 2 * l) - 128
-                    w0 = w0 + 256 * j
-                    acc = psum.tile([P, 512], F32, name="acc", tag="acc")
-                    for i, u in enumerate(range(u0, u1)):
-                        s = s0 + u
-                        for h in range(2):
-                            lo = 128 * s + 64 - 64 * h
-                            nc.tensor.matmul_mx(
-                                out=acc[:, i * n:(i + 1) * n],
-                                lhsT=xc[:, lo:lo + 128].bitcast(FP8X4),
-                                lhsT_scale=xs[:, lo:lo + 128],
-                                rhs=pc[:, h, w0:w0 + n].bitcast(FP8X4),
-                                rhs_scale=ps[:, h, w0:w0 + n],
-                                start=(h == 0),
-                                stop=(h == 1),
-                            )
-                    nu = u1 - u0
-                    src = acc[:, 0:nu * n].rearrange("p (u n) -> p u n", n=n)[:, :, off:off + GL * d]
-                    src = src.rearrange("p u (g m) -> p g u m", m=d)
-                    ca, cb = cl + u0 * d, cl + u1 * d
-                    a, b = [(a, b) for a, b in segs if a <= ca and cb <= b][0]
-                    seg = o[:, GL * a:GL * b].rearrange("p (g k) -> p g k", g=GL)
-                    dst = seg[:, :, ca - a:cb - a].rearrange("p g (u m) -> p g u m", m=d)
-                    if VTURN[c] > 0 and gi % VTURN[c] == VTURN[c] - 1:
+        bank = 0
+        stage = 0
+        for wi, (st, l, q0, q1, n, off, k) in enumerate(wins):
+            while ready < min(len(slots) - 1, k + 2):
+                ready = ready + 1
+                prep_copy(ready + 1)
+                prep_quant(ready)
+            d = 2 * l + 1
+            cl = c_of(l)
+            pc, ps = slots[k]["codes"]
+            per = 512 // n
+            for u0 in range(0, d, per):
+                u1 = min(u0 + per, d)
+                acc = psum.tile([P, 512], F32, name="acc", tag="acc")
+                for i, u in enumerate(range(u0, u1)):
+                    for h in range(2):
+                        lo = 128 * (l * l + u) + 64 - 64 * h
+                        nc.tensor.matmul_mx(
+                            out=acc[:, i * n:(i + 1) * n],
+                            lhsT=xc[:, lo:lo + 128].bitcast(FP8X4),
+                            lhsT_scale=xs[:, lo:lo + 128],
+                            rhs=pc[:, h, :].bitcast(FP8X4),
+                            rhs_scale=ps[:, h, :],
+                            start=(h == 0),
+                            stop=(h == 1),
+                        )
+                nu = u1 - u0
+                cuts = [q0] + [q for q in range(RING, NQ, RING) if q0 < q and q < q1] + [q1]
+                use_v = st > 0 and bank % 4 == 3
+                for qa, qb in zip(cuts[:-1], cuts[1:]):
+                    a = off + (qa - q0) * d
+                    src = acc[:, 0:nu * n].rearrange("p (u n) -> p u n", n=n)[:, :, a:a + (qb - qa) * d]
+                    src = src.rearrange("p u (q m) -> p q u m", m=d)
+                    r = qa % RING
+                    dst = ring[:, r * C:(r + qb - qa) * C].rearrange("p (q c) -> p q c", c=C)
+                    dst = dst[:, :, cl + u0 * d:cl + u1 * d].rearrange("p q (u m) -> p q u m", m=d)
+                    if use_v:
                         nc.vector.tensor_scalar_mul(out=dst, in0=src, scalar1=SCALE)
                     else:
                         nc.scalar.activation(out=dst, in_=src, func=mybir.ActivationFunctionType.Copy, scale=SCALE)
-                    if ca == a:
-                        nc.sync.dma_start(out=out_v[:, GL * c:GL * c + GL, a:b], in_=seg)
+                bank = bank + 1
+            if wi + 1 == len(wins) or wins[wi + 1][0] > st:
+                r = STEP * st % RING
+                nc.sync.dma_start(
+                    out=out_v[:, STEP * st:STEP * st + STEP, :],
+                    in_=ring[:, r * C:(r + STEP) * C].rearrange("p (q c) -> p q c", c=C),
+                )

@@ -13,11 +13,12 @@ P = 128
 B, F, G, S2, LMAX = 64, 512, 128, 64, 7
 C = 680
 NQ = 64
-RING = 32
+RING = 36
 STEP = 8
 NSTAGE = NQ // STEP
 SCALE = 1.0 / (512.0 ** 0.5)
 FLOPS = 2 * F * B * G * C
+XCUT = 25
 XG0 = RING * C - S2 * B * 2
 
 
@@ -31,13 +32,12 @@ def q_windows(l):
     out = []
     q = 0
     while q < NQ:
-        rem = NQ - q
-        if rem > 2 * n and rem <= min(24, 256 // d):
-            out.append((q, NQ, 256))
-            q = NQ
-        else:
-            out.append((q, min(q + n, NQ), 128))
-            q = min(q + n, NQ)
+        m = n
+        if l == 6 and q == 18:
+            m = 256 // d
+        m = min(m, NQ - q)
+        out.append((q, q + m, 128 if m <= n else 256))
+        q = q + m
     return out
 
 
@@ -49,7 +49,7 @@ def tile_s2conv_pa_kernel(tc, x, psi, out):
 
     with ExitStack() as ctx:
         keep = ctx.enter_context(tc.tile_pool(name="keep", bufs=1))
-        cpool = ctx.enter_context(tc.tile_pool(name="cpool", bufs=14))
+        cpool = ctx.enter_context(tc.tile_pool(name="cpool", bufs=12))
         psum = ctx.enter_context(tc.psum_pool(name="psum", bufs=8))
         ctx.enter_context(tc.manual_schedule())
 
@@ -72,8 +72,8 @@ def tile_s2conv_pa_kernel(tc, x, psi, out):
         nc.vector.memset(xsi[:, 0:2048].rearrange("p (k w) -> p k w", w=32)[:, :, 0:16], 0)
         nc.vector.memset(xsi[:, 2048:2064], 0)
         for gp in gps:
-            nc.gpsimd.memset(gp[:], 0.0)
-        nc.gpsimd.memset(gpw[:], 0.0)
+            nc.gpsimd.memset(gp[:, :, 96:128, :], 0.0)
+        nc.gpsimd.memset(gpw[:, :, 240:256, :], 0.0)
 
         xg = ring[:, XG0:RING * C].bitcast(BF16).rearrange("p (s b t) -> p s b t", s=S2, b=B)
         xraw = raw[:, 64:128, :]
@@ -81,19 +81,11 @@ def tile_s2conv_pa_kernel(tc, x, psi, out):
             nc.sync.dma_start(out=xraw[:, b0:b0 + n, :], in_=x_v[:, b0:b0 + n, :])
         for g0 in range(0, 64, 16):
             nc.sync.dma_start(out=raw[:, g0:g0 + 16, :], in_=psi_v[:, g0:g0 + 16, :])
-        for b0 in (0, 16, 32, 48):
-            if b0 == 48:
-                parts = (("v", 0, 4), ("s", 4, 4), ("s", 8, 4), ("v", 12, 4))
-            else:
-                parts = (("v", 0, 10), ("s", 10, 6))
-            for eng, a, n in parts:
-                lo = b0 + a
-                src = xraw[:, lo:lo + n, :].rearrange("p b (t s) -> p b s t", t=4)
-                dst = xg[:, :, lo:lo + n, :].rearrange("p s b t -> p b s t")
-                if eng == "v":
-                    nc.vector.tensor_copy(out=dst, in_=src)
-                else:
-                    nc.scalar.copy(out=dst, in_=src)
+        for b0, n in ((0, 16), (16, 16), (32, 16), (48, 8), (56, 4), (60, 4)):
+            src = xraw[:, b0:b0 + n, :].rearrange("p b (t s) -> p b s t", t=4)
+            dst = xg[:, :, b0:b0 + n, :].rearrange("p s b t -> p b s t")
+            nc.vector.tensor_copy(out=dst[:, :, XCUT:S2, :], in_=src[:, :, XCUT:S2, :])
+            nc.scalar.copy(out=dst[:, :, 0:XCUT, :], in_=src[:, :, 0:XCUT, :])
         for g0 in range(64, 128, 16):
             nc.sync.dma_start(out=raw[:, g0:g0 + 16, :], in_=psi_v[:, g0:g0 + 16, :])
 
@@ -131,7 +123,11 @@ def tile_s2conv_pa_kernel(tc, x, psi, out):
                 d = 2 * l + 1
                 s0 = l * l
                 dst = gp[:, :, off:off + (q1 - q0) * d, :].rearrange("p h (q m) t -> p h q m t", m=d)
-                nc.vector.tensor_copy(out=dst, in_=rawv[:, :, q0:q1, s0:s0 + d, :])
+                src = rawv[:, :, q0:q1, s0:s0 + d, :]
+                if k < 3:
+                    nc.scalar.copy(out=dst, in_=src)
+                else:
+                    nc.vector.tensor_copy(out=dst, in_=src)
 
         def quant_slot(k):
             slot = slots[k]
@@ -148,8 +144,6 @@ def tile_s2conv_pa_kernel(tc, x, psi, out):
                 in_=slot["gp"][:].rearrange("p h w t -> p (h w t)"),
             )
 
-        copied = 0
-        quanted = 0
         xdone = []
 
         def prep_copy(k):
@@ -164,14 +158,13 @@ def tile_s2conv_pa_kernel(tc, x, psi, out):
                         xdone.append(l)
                 quant_slot(k)
 
-        qx(49, 60)
         copy_slot(0)
-        qx(60, 64)
+        qx(49, 64)
         xdone.append(7)
-        quant_slot(0)
         copy_slot(1)
-        prep_quant(1)
+        quant_slot(0)
         copy_slot(2)
+        prep_quant(1)
         ready = 1
 
         bank = 0
@@ -201,7 +194,7 @@ def tile_s2conv_pa_kernel(tc, x, psi, out):
                             stop=(h == 1),
                         )
                 nu = u1 - u0
-                cuts = [q0] + [q for q in range(RING, NQ, RING) if q0 < q and q < q1] + [q1]
+                cuts = [q0] + [q for q in range(RING, NQ, RING) if q0 < q < q1] + [q1]
                 use_v = st > 0 and bank % 4 == 3
                 for qa, qb in zip(cuts[:-1], cuts[1:]):
                     a = off + (qa - q0) * d
@@ -216,8 +209,10 @@ def tile_s2conv_pa_kernel(tc, x, psi, out):
                         nc.scalar.activation(out=dst, in_=src, func=mybir.ActivationFunctionType.Copy, scale=SCALE)
                 bank = bank + 1
             if wi + 1 == len(wins) or wins[wi + 1][0] > st:
-                r = STEP * st % RING
-                nc.sync.dma_start(
-                    out=out_v[:, STEP * st:STEP * st + STEP, :],
-                    in_=ring[:, r * C:(r + STEP) * C].rearrange("p (q c) -> p q c", c=C),
-                )
+                cuts = [STEP * st] + [q for q in range(RING, NQ, RING) if STEP * st < q < STEP * st + STEP] + [STEP * st + STEP]
+                for qa, qb in zip(cuts[:-1], cuts[1:]):
+                    r = qa % RING
+                    nc.sync.dma_start(
+                        out=out_v[:, qa:qb, :],
+                        in_=ring[:, r * C:(r + qb - qa) * C].rearrange("p (q c) -> p q c", c=C),
+                    )

@@ -41,6 +41,19 @@ def q_windows(l):
     return out
 
 
+def u_groups(l, per):
+    d = 2 * l + 1
+    first = [u for u in range(1, min(per + 1, d)) if (c_of(l) + u * d) % 4 == 0]
+    u0 = 0
+    groups = []
+    if len(first) > 0 and (d - first[0] + per - 1) // per < (d + per - 1) // per:
+        groups.append((0, first[0]))
+        u0 = first[0]
+    for u in range(u0, d, per):
+        groups.append((u, min(u + per, d)))
+    return groups
+
+
 def tile_s2conv_pa_kernel(tc, x, psi, out):
     nc = tc.nc
     x_v = x.rearrange("b (p t) s -> p b (t s)", t=4)
@@ -178,8 +191,7 @@ def tile_s2conv_pa_kernel(tc, x, psi, out):
             cl = c_of(l)
             pc, ps = slots[k]["codes"]
             per = 512 // n
-            for u0 in range(0, d, per):
-                u1 = min(u0 + per, d)
+            for u0, u1 in u_groups(l, per):
                 acc = psum.tile([P, 512], F32, name="acc", tag="acc")
                 for i, u in enumerate(range(u0, u1)):
                     for h in range(2):

@@ -14,8 +14,9 @@ B, F, G, S2, LMAX = 64, 512, 128, 64, 7
 C = 680
 NQ = 64
 RING = 36
-STEP = 8
-NSTAGE = NQ // STEP
+STORE = 2
+REACH = 24
+NARROW = 24
 SCALE = 1.0 / (512.0 ** 0.5)
 FLOPS = 2 * F * B * G * C
 XCUT = 25
@@ -28,16 +29,15 @@ def c_of(l):
 
 def q_windows(l):
     d = 2 * l + 1
-    n = min(24, 128 // d)
     out = []
     q = 0
     while q < NQ:
-        m = n
-        if l == 6 and q == 18:
-            m = 256 // d
-        m = min(m, NQ - q)
-        out.append((q, q + m, 128 if m <= n else 256))
-        q = q + m
+        n = 128
+        if l >= 4 and q >= NARROW and (NQ - q) * d > 128:
+            n = 256
+        q1 = min(q + min(REACH, n // d), NQ)
+        out.append((q, q1, n))
+        q = q1
     return out
 
 
@@ -62,7 +62,8 @@ def tile_s2conv_pa_kernel(tc, x, psi, out):
 
     with ExitStack() as ctx:
         keep = ctx.enter_context(tc.tile_pool(name="keep", bufs=1))
-        cpool = ctx.enter_context(tc.tile_pool(name="cpool", bufs=12))
+        narrow = ctx.enter_context(tc.tile_pool(name="narrow", bufs=6))
+        wide = ctx.enter_context(tc.tile_pool(name="wide", bufs=4))
         psum = ctx.enter_context(tc.psum_pool(name="psum", bufs=8))
         ctx.enter_context(tc.manual_schedule())
 
@@ -71,12 +72,9 @@ def tile_s2conv_pa_kernel(tc, x, psi, out):
         raw = keep.tile([P, G, 256], BF16, name="raw", align_bytes=64)
         ring = keep.tile([P, RING * C], F32, name="ring", align_bytes=64)
         gps = []
-        for i in range(4):
-            gp = keep.tile([P, 2, 128, 4], BF16, name="gp%d" % i, align_bytes=64)
+        for i in range(3):
+            gp = keep.tile([P, 2048], BF16, name="gp%d" % i, align_bytes=64)
             gps.append(gp)
-        gpw = keep.tile([P, 2, 256, 4], BF16, name="gpw", align_bytes=64)
-        pcw = keep.tile([P, 2, 256], U32, name="pcw", align_bytes=64)
-        psw = keep.tile([P, 2, 256], U8, name="psw", align_bytes=64)
 
         xci = xc[:].bitcast(I32)
         xsi = xs[:].bitcast(I32)
@@ -85,8 +83,8 @@ def tile_s2conv_pa_kernel(tc, x, psi, out):
         nc.vector.memset(xsi[:, 0:2048].rearrange("p (k w) -> p k w", w=32)[:, :, 0:16], 0)
         nc.vector.memset(xsi[:, 2048:2064], 0)
         for gp in gps:
-            nc.gpsimd.memset(gp[:, :, 96:128, :], 0.0)
-        nc.gpsimd.memset(gpw[:, :, 240:256, :], 0.0)
+            for a, b in ((384, 512), (864, 1024), (1888, 2048)):
+                nc.gpsimd.memset(gp[:, a:b], 0.0)
 
         xg = ring[:, XG0:RING * C].bitcast(BF16).rearrange("p (s b t) -> p s b t", s=S2, b=B)
         xraw = raw[:, 64:128, :]
@@ -114,30 +112,32 @@ def tile_s2conv_pa_kernel(tc, x, psi, out):
         todo = [q_windows(l) for l in range(LMAX + 1)]
         wins = []
         slots = []
-        for st in range(NSTAGE):
-            for l in range(LMAX, -1, -1):
-                while len(todo[l]) > 0 and todo[l][0][0] < STEP * (st + 1):
-                    q0, q1, n = todo[l].pop(0)
-                    off = 0
-                    if l == 0:
-                        off = 3 * (q1 - q0)
-                        slots[-1]["parts"].append((l, q0, q1, off))
-                    else:
-                        slots.append({"parts": [(l, q0, q1, off)], "n": n, "k": len(slots)})
-                    wins.append((st, l, q0, q1, n, off, len(slots) - 1))
+        cover = [0] * (LMAX + 1)
+        while min(cover) < NQ:
+            l = max([i for i in range(LMAX + 1) if cover[i] == min(cover)])
+            q0, q1, n = [w for w in todo[l] if w[0] == cover[l]][0]
+            cover[l] = q1
+            if l == 0:
+                off = 3 * (q1 - q0)
+                slots[-1]["parts"].append((l, q0, q1, off))
+            else:
+                off = 0
+                slots.append({"parts": [(l, q0, q1, off)], "n": n, "k": len(slots)})
+            wins.append((min(cover), l, q0, q1, n, off, len(slots) - 1))
 
         rawv = raw[:].rearrange("p (q h) (t s) -> p h q s t", h=2, t=4)
 
         def copy_slot(k):
             slot = slots[k]
-            gp = gpw if slot["n"] == 256 else gps[k % len(gps)]
+            n = slot["n"]
+            gp = gps[k % len(gps)][:, 0:8 * n].rearrange("p (h w t) -> p h w t", h=2, t=4)
             slot["gp"] = gp
             for l, q0, q1, off in slot["parts"]:
                 d = 2 * l + 1
                 s0 = l * l
                 dst = gp[:, :, off:off + (q1 - q0) * d, :].rearrange("p h (q m) t -> p h q m t", m=d)
                 src = rawv[:, :, q0:q1, s0:s0 + d, :]
-                if k < 3:
+                if k < 4:
                     nc.scalar.copy(out=dst, in_=src)
                 else:
                     nc.vector.tensor_copy(out=dst, in_=src)
@@ -146,25 +146,36 @@ def tile_s2conv_pa_kernel(tc, x, psi, out):
             slot = slots[k]
             n = slot["n"]
             if n == 256:
-                pc, ps = pcw, psw
+                pc = wide.tile([P, 2, 256], U32, name="pcw", tag="pcw", align_bytes=64)
+                ps = wide.tile([P, 2, 256], U8, name="psw", tag="psw", align_bytes=64)
             else:
-                pc = cpool.tile([P, 2, 128], U32, name="pc", tag="pc", align_bytes=64)
-                ps = cpool.tile([P, 2, 128], U8, name="ps", tag="ps", align_bytes=64)
+                pc = narrow.tile([P, 2, 128], U32, name="pc", tag="pc", align_bytes=64)
+                ps = narrow.tile([P, 2, 128], U8, name="ps", tag="ps", align_bytes=64)
             slot["codes"] = (pc, ps)
             nc.vector.quantize_mx(
                 out=pc[:].rearrange("p h w -> p (h w)").bitcast(FP8X4),
                 scales=ps[:].rearrange("p h w -> p (h w)"),
-                in_=slot["gp"][:].rearrange("p h w t -> p (h w t)"),
+                in_=slot["gp"].rearrange("p h w t -> p (h w t)"),
             )
 
+        banks = []
+        first = []
+        for w in wins:
+            if w[6] == len(first):
+                first.append(len(banks))
+            for u0, u1 in u_groups(w[1], 512 // w[4]):
+                banks.append((w, u0, u1))
+
+        before = {}
+        for k in range(len(slots)):
+            before.setdefault(max(0, first[k] - 8), []).append(("copy", k))
+            before.setdefault(max(0, first[k] - 4), []).append(("quant", k))
         xdone = []
 
-        def prep_copy(k):
-            if k < len(slots):
+        def run_step(kind, k):
+            if kind == "copy":
                 copy_slot(k)
-
-        def prep_quant(k):
-            if k < len(slots):
+            else:
                 for l, q0, q1, off in slots[k]["parts"]:
                     if l not in xdone:
                         qx(l * l, (l + 1) ** 2)
@@ -177,54 +188,55 @@ def tile_s2conv_pa_kernel(tc, x, psi, out):
         copy_slot(1)
         quant_slot(0)
         copy_slot(2)
-        prep_quant(1)
-        ready = 1
+        run_step("quant", 1)
+        for step in before[0]:
+            if step not in (("copy", 0), ("quant", 0), ("copy", 1), ("quant", 1), ("copy", 2)):
+                run_step(*step)
+        for i in before:
+            before[i] = [z for z in before[i] if z not in (("copy", 0), ("quant", 0), ("copy", 1), ("quant", 1), ("copy", 2))]
 
-        bank = 0
-        stage = 0
-        for wi, (st, l, q0, q1, n, off, k) in enumerate(wins):
-            while ready < min(len(slots) - 1, k + 2):
-                ready = ready + 1
-                prep_copy(ready + 1)
-                prep_quant(ready)
+        stored = 0
+        for bi, (w, u0, u1) in enumerate(banks):
+            fin, l, q0, q1, n, off, k = w
+            if bi > 0:
+                for step in before.get(bi, []):
+                    run_step(*step)
             d = 2 * l + 1
             cl = c_of(l)
             pc, ps = slots[k]["codes"]
-            per = 512 // n
-            for u0, u1 in u_groups(l, per):
-                acc = psum.tile([P, 512], F32, name="acc", tag="acc")
-                for i, u in enumerate(range(u0, u1)):
-                    for h in range(2):
-                        lo = 128 * (l * l + u) + 64 - 64 * h
-                        nc.tensor.matmul_mx(
-                            out=acc[:, i * n:(i + 1) * n],
-                            lhsT=xc[:, lo:lo + 128].bitcast(FP8X4),
-                            lhsT_scale=xs[:, lo:lo + 128],
-                            rhs=pc[:, h, :].bitcast(FP8X4),
-                            rhs_scale=ps[:, h, :],
-                            start=(h == 0),
-                            stop=(h == 1),
-                        )
-                nu = u1 - u0
-                cuts = [q0] + [q for q in range(RING, NQ, RING) if q0 < q < q1] + [q1]
-                use_v = st > 0 and bank % 4 == 3
-                for qa, qb in zip(cuts[:-1], cuts[1:]):
-                    a = off + (qa - q0) * d
-                    src = acc[:, 0:nu * n].rearrange("p (u n) -> p u n", n=n)[:, :, a:a + (qb - qa) * d]
-                    src = src.rearrange("p u (q m) -> p q u m", m=d)
-                    r = qa % RING
-                    dst = ring[:, r * C:(r + qb - qa) * C].rearrange("p (q c) -> p q c", c=C)
-                    dst = dst[:, :, cl + u0 * d:cl + u1 * d].rearrange("p q (u m) -> p q u m", m=d)
-                    if use_v:
-                        nc.vector.tensor_scalar_mul(out=dst, in0=src, scalar1=SCALE)
-                    else:
-                        nc.scalar.activation(out=dst, in_=src, func=mybir.ActivationFunctionType.Copy, scale=SCALE)
-                bank = bank + 1
-            if wi + 1 == len(wins) or wins[wi + 1][0] > st:
-                cuts = [STEP * st] + [q for q in range(RING, NQ, RING) if STEP * st < q < STEP * st + STEP] + [STEP * st + STEP]
+            acc = psum.tile([P, 512], F32, name="acc", tag="acc")
+            for i, u in enumerate(range(u0, u1)):
+                for h in range(2):
+                    lo = 128 * (l * l + u) + 64 - 64 * h
+                    nc.tensor.matmul_mx(
+                        out=acc[:, i * n:(i + 1) * n],
+                        lhsT=xc[:, lo:lo + 128].bitcast(FP8X4),
+                        lhsT_scale=xs[:, lo:lo + 128],
+                        rhs=pc[:, h, :].bitcast(FP8X4),
+                        rhs_scale=ps[:, h, :],
+                        start=(h == 0),
+                        stop=(h == 1),
+                    )
+            nu = u1 - u0
+            cuts = [q0] + [q for q in range(RING, NQ, RING) if q0 < q < q1] + [q1]
+            use_v = stored > 0 and bi % 4 == 3
+            for qa, qb in zip(cuts[:-1], cuts[1:]):
+                a = off + (qa - q0) * d
+                src = acc[:, 0:nu * n].rearrange("p (u n) -> p u n", n=n)[:, :, a:a + (qb - qa) * d]
+                src = src.rearrange("p u (q m) -> p q u m", m=d)
+                r = qa % RING
+                dst = ring[:, r * C:(r + qb - qa) * C].rearrange("p (q c) -> p q c", c=C)
+                dst = dst[:, :, cl + u0 * d:cl + u1 * d].rearrange("p q (u m) -> p q u m", m=d)
+                if use_v:
+                    nc.vector.tensor_scalar_mul(out=dst, in0=src, scalar1=SCALE)
+                else:
+                    nc.scalar.activation(out=dst, in_=src, func=mybir.ActivationFunctionType.Copy, scale=SCALE)
+            if u1 == d and (fin - stored >= STORE or fin == NQ):
+                cuts = [stored] + [q for q in range(RING, NQ, RING) if stored < q < fin] + [fin]
                 for qa, qb in zip(cuts[:-1], cuts[1:]):
                     r = qa % RING
                     nc.sync.dma_start(
                         out=out_v[:, qa:qb, :],
                         in_=ring[:, r * C:(r + qb - qa) * C].rearrange("p (q c) -> p q c", c=C),
                     )
+                stored = fin

@@ -15,8 +15,7 @@ C = 680
 NQ = 64
 RING = 36
 STORE = 2
-REACH = 24
-NARROW = 24
+REACH = 25
 SCALE = 1.0 / (512.0 ** 0.5)
 FLOPS = 2 * F * B * G * C
 XCUT = 25
@@ -33,7 +32,7 @@ def q_windows(l):
     q = 0
     while q < NQ:
         n = 128
-        if l >= 4 and q >= NARROW and (NQ - q) * d > 128:
+        if l >= 4 and q > 0 and (NQ - q) * d > 128:
             n = 256
         q1 = min(q + min(REACH, n // d), NQ)
         out.append((q, q1, n))
@@ -137,7 +136,7 @@ def tile_s2conv_pa_kernel(tc, x, psi, out):
                 s0 = l * l
                 dst = gp[:, :, off:off + (q1 - q0) * d, :].rearrange("p h (q m) t -> p h q m t", m=d)
                 src = rawv[:, :, q0:q1, s0:s0 + d, :]
-                if k < 4:
+                if k < 3:
                     nc.scalar.copy(out=dst, in_=src)
                 else:
                     nc.vector.tensor_copy(out=dst, in_=src)

@@ -19,7 +19,8 @@ REACH = 25
 SCALE = 1.0 / (512.0 ** 0.5)
 FLOPS = 2 * F * B * G * C
 XCUT = 25
-XG0 = RING * C - S2 * B * 2
+CP = 704
+XG0 = RING * CP - S2 * B * 2
 
 
 def c_of(l):
@@ -62,14 +63,14 @@ def tile_s2conv_pa_kernel(tc, x, psi, out):
     with ExitStack() as ctx:
         keep = ctx.enter_context(tc.tile_pool(name="keep", bufs=1))
         narrow = ctx.enter_context(tc.tile_pool(name="narrow", bufs=6))
-        wide = ctx.enter_context(tc.tile_pool(name="wide", bufs=4))
+        wide = ctx.enter_context(tc.tile_pool(name="wide", bufs=3))
         psum = ctx.enter_context(tc.psum_pool(name="psum", bufs=8))
         ctx.enter_context(tc.manual_schedule())
 
         xc = keep.tile([P, 64 + 128 * S2], U32, name="xc", align_bytes=64)
         xs = keep.tile([P, 64 + 128 * S2], U8, name="xs", align_bytes=64)
         raw = keep.tile([P, G, 256], BF16, name="raw", align_bytes=64)
-        ring = keep.tile([P, RING * C], F32, name="ring", align_bytes=64)
+        ring = keep.tile([P, RING * CP], F32, name="ring", align_bytes=256)
         gps = []
         for i in range(3):
             gp = keep.tile([P, 2048], BF16, name="gp%d" % i, align_bytes=64)
@@ -85,7 +86,7 @@ def tile_s2conv_pa_kernel(tc, x, psi, out):
             for a, b in ((384, 512), (864, 1024), (1888, 2048)):
                 nc.gpsimd.memset(gp[:, a:b], 0.0)
 
-        xg = ring[:, XG0:RING * C].bitcast(BF16).rearrange("p (s b t) -> p s b t", s=S2, b=B)
+        xg = ring[:, XG0:RING * CP].bitcast(BF16).rearrange("p (s b t) -> p s b t", s=S2, b=B)
         xraw = raw[:, 64:128, :]
         for b0, n in ((0, 16), (16, 16), (32, 16), (48, 8), (56, 4), (60, 4)):
             nc.sync.dma_start(out=xraw[:, b0:b0 + n, :], in_=x_v[:, b0:b0 + n, :])
@@ -224,7 +225,7 @@ def tile_s2conv_pa_kernel(tc, x, psi, out):
                 src = acc[:, 0:nu * n].rearrange("p (u n) -> p u n", n=n)[:, :, a:a + (qb - qa) * d]
                 src = src.rearrange("p u (q m) -> p q u m", m=d)
                 r = qa % RING
-                dst = ring[:, r * C:(r + qb - qa) * C].rearrange("p (q c) -> p q c", c=C)
+                dst = ring[:, r * CP:(r + qb - qa) * CP].rearrange("p (q c) -> p q c", c=CP)
                 dst = dst[:, :, cl + u0 * d:cl + u1 * d].rearrange("p q (u m) -> p q u m", m=d)
                 if use_v:
                     nc.vector.tensor_scalar_mul(out=dst, in0=src, scalar1=SCALE)
@@ -236,6 +237,6 @@ def tile_s2conv_pa_kernel(tc, x, psi, out):
                     r = qa % RING
                     nc.sync.dma_start(
                         out=out_v[:, qa:qb, :],
-                        in_=ring[:, r * C:(r + qb - qa) * C].rearrange("p (q c) -> p q c", c=C),
+                        in_=ring[:, r * CP:(r + qb - qa) * CP].rearrange("p (q c) -> p q c", c=CP)[:, :, 0:C],
                     )
                 stored = fin

from contextlib import ExitStack

import concourse.mybir as mybir

FP8X4 = mybir.dt.float8_e4m3fn_x4
BF16 = mybir.dt.bfloat16
F32 = mybir.dt.float32
U32 = mybir.dt.uint32
U8 = mybir.dt.uint8
I32 = mybir.dt.int32

P = 128
B, F, G, S2, LMAX = 64, 512, 128, 64, 7
C = 680
NQ = 64
RING = 36
STORE = 2
REACH = 25
SCALE = 1.0 / (512.0 ** 0.5)
FLOPS = 2 * F * B * G * C
XCUT = 25
CP = 704
XG0 = RING * CP - S2 * B * 2


def c_of(l):
    return sum((2 * k + 1) ** 2 for k in range(l))


def q_windows(l):
    d = 2 * l + 1
    out = []
    q = 0
    while q < NQ:
        n = 128
        if l >= 4 and q > 0 and (NQ - q) * d > 128:
            n = 256
        q1 = min(q + min(REACH, n // d), NQ)
        out.append((q, q1, n))
        q = q1
    return out


def u_groups(l, per):
    d = 2 * l + 1
    first = [u for u in range(1, min(per + 1, d)) if (c_of(l) + u * d) % 4 == 0]
    u0 = 0
    groups = []
    if len(first) > 0 and (d - first[0] + per - 1) // per < (d + per - 1) // per:
        groups.append((0, first[0]))
        u0 = first[0]
    for u in range(u0, d, per):
        groups.append((u, min(u + per, d)))
    return groups


def tile_s2conv_pa_kernel(tc, x, psi, out):
    nc = tc.nc
    x_v = x.rearrange("b (p t) s -> p b (t s)", t=4)
    psi_v = psi.rearrange("g (p t) s -> p g (t s)", t=4)
    out_v = out.flatten_outer_dims().rearrange("(q p) c -> p q c", p=P)

    with ExitStack() as ctx:
        keep = ctx.enter_context(tc.tile_pool(name="keep", bufs=1))
        narrow = ctx.enter_context(tc.tile_pool(name="narrow", bufs=6))
        wide = ctx.enter_context(tc.tile_pool(name="wide", bufs=3))
        psum = ctx.enter_context(tc.psum_pool(name="psum", bufs=8))
        ctx.enter_context(tc.manual_schedule())

        xc = keep.tile([P, 64 + 128 * S2], U32, name="xc", align_bytes=64)
        xs = keep.tile([P, 64 + 128 * S2], U8, name="xs", align_bytes=64)
        raw = keep.tile([P, G, 256], BF16, name="raw", align_bytes=64)
        ring = keep.tile([P, RING * CP], F32, name="ring", align_bytes=256)
        gps = []
        for i in range(3):
            gp = keep.tile([P, 2048], BF16, name="gp%d" % i, align_bytes=64)
            gps.append(gp)

        xci = xc[:].bitcast(I32)
        xsi = xs[:].bitcast(I32)
        nc.vector.memset(xci[:, 0:8192].rearrange("p (k w) -> p k w", w=128)[:, :, 0:64], 0)
        nc.vector.memset(xci[:, 8192:8256], 0)
        nc.vector.memset(xsi[:, 0:2048].rearrange("p (k w) -> p k w", w=32)[:, :, 0:16], 0)
        nc.vector.memset(xsi[:, 2048:2064], 0)
        for gp in gps:
            for a, b in ((384, 512), (864, 1024), (1888, 2048)):
                nc.gpsimd.memset(gp[:, a:b], 0.0)

        xg = ring[:, XG0:RING * CP].bitcast(BF16).rearrange("p (s b t) -> p s b t", s=S2, b=B)
        xraw = raw[:, 64:128, :]
        for b0, n in ((0, 16), (16, 16), (32, 16), (48, 8), (56, 4), (60, 4)):
            nc.sync.dma_start(out=xraw[:, b0:b0 + n, :], in_=x_v[:, b0:b0 + n, :])
        for g0 in range(0, 64, 16):
            nc.sync.dma_start(out=raw[:, g0:g0 + 16, :], in_=psi_v[:, g0:g0 + 16, :])
        for b0, n in ((0, 16), (16, 16), (32, 16), (48, 8), (56, 4), (60, 4)):
            src = xraw[:, b0:b0 + n, :].rearrange("p b (t s) -> p b s t", t=4)
            dst = xg[:, :, b0:b0 + n, :].rearrange("p s b t -> p b s t")
            nc.vector.tensor_copy(out=dst[:, :, XCUT:S2, :], in_=src[:, :, XCUT:S2, :])
            nc.scalar.copy(out=dst[:, :, 0:XCUT, :], in_=src[:, :, 0:XCUT, :])
        for g0 in range(64, 128, 16):
            nc.sync.dma_start(out=raw[:, g0:g0 + 16, :], in_=psi_v[:, g0:g0 + 16, :])

        def qx(s0, s1):
            for s in range(s0, s1):
                lo = 128 * s + 64
                nc.vector.quantize_mx(
                    out=xc[:, lo:lo + 64].bitcast(FP8X4),
                    scales=xs[:, lo:lo + 64],
                    in_=xg[:, s].rearrange("p b t -> p (b t)"),
                )

        todo = [q_windows(l) for l in range(LMAX + 1)]
        wins = []
        slots = []
        cover = [0] * (LMAX + 1)
        while min(cover) < NQ:
            l = max([i for i in range(LMAX + 1) if cover[i] == min(cover)])
            q0, q1, n = [w for w in todo[l] if w[0] == cover[l]][0]
            cover[l] = q1
            if l == 0:
                off = 3 * (q1 - q0)
                slots[-1]["parts"].append((l, q0, q1, off))
            else:
                off = 0
                slots.append({"parts": [(l, q0, q1, off)], "n": n, "k": len(slots)})
            wins.append((min(cover), l, q0, q1, n, off, len(slots) - 1))

        rawv = raw[:].rearrange("p (q h) (t s) -> p h q s t", h=2, t=4)

        def copy_slot(k):
            slot = slots[k]
            n = slot["n"]
            gp = gps[k % len(gps)][:, 0:8 * n].rearrange("p (h w t) -> p h w t", h=2, t=4)
            slot["gp"] = gp
            for l, q0, q1, off in slot["parts"]:
                d = 2 * l + 1
                s0 = l * l
                dst = gp[:, :, off:off + (q1 - q0) * d, :].rearrange("p h (q m) t -> p h q m t", m=d)
                src = rawv[:, :, q0:q1, s0:s0 + d, :]
                if k < 3:
                    nc.scalar.copy(out=dst, in_=src)
                else:
                    nc.vector.tensor_copy(out=dst, in_=src)

        def quant_slot(k):
            slot = slots[k]
            n = slot["n"]
            if n == 256:
                pc = wide.tile([P, 2, 256], U32, name="pcw", tag="pcw", align_bytes=64)
                ps = wide.tile([P, 2, 256], U8, name="psw", tag="psw", align_bytes=64)
            else:
                pc = narrow.tile([P, 2, 128], U32, name="pc", tag="pc", align_bytes=64)
                ps = narrow.tile([P, 2, 128], U8, name="ps", tag="ps", align_bytes=64)
            slot["codes"] = (pc, ps)
            nc.vector.quantize_mx(
                out=pc[:].rearrange("p h w -> p (h w)").bitcast(FP8X4),
                scales=ps[:].rearrange("p h w -> p (h w)"),
                in_=slot["gp"].rearrange("p h w t -> p (h w t)"),
            )

        banks = []
        first = []
        for w in wins:
            if w[6] == len(first):
                first.append(len(banks))
            for u0, u1 in u_groups(w[1], 512 // w[4]):
                banks.append((w, u0, u1))

        before = {}
        for k in range(len(slots)):
            before.setdefault(max(0, first[k] - 8), []).append(("copy", k))
            before.setdefault(max(0, first[k] - 4), []).append(("quant", k))
        xdone = []

        def run_step(kind, k):
            if kind == "copy":
                copy_slot(k)
            else:
                for l, q0, q1, off in slots[k]["parts"]:
                    if l not in xdone:
                        qx(l * l, (l + 1) ** 2)
                        xdone.append(l)
                quant_slot(k)

        copy_slot(0)
        qx(49, 64)
        xdone.append(7)
        copy_slot(1)
        quant_slot(0)
        copy_slot(2)
        run_step("quant", 1)
        for step in before[0]:
            if step not in (("copy", 0), ("quant", 0), ("copy", 1), ("quant", 1), ("copy", 2)):
                run_step(*step)
        for i in before:
            before[i] = [z for z in before[i] if z not in (("copy", 0), ("quant", 0), ("copy", 1), ("quant", 1), ("copy", 2))]

        stored = 0
        for bi, (w, u0, u1) in enumerate(banks):
            fin, l, q0, q1, n, off, k = w
            if bi > 0:
                for step in before.get(bi, []):
                    run_step(*step)
            d = 2 * l + 1
            cl = c_of(l)
            pc, ps = slots[k]["codes"]
            acc = psum.tile([P, 512], F32, name="acc", tag="acc")
            for i, u in enumerate(range(u0, u1)):
                for h in range(2):
                    lo = 128 * (l * l + u) + 64 - 64 * h
                    nc.tensor.matmul_mx(
                        out=acc[:, i * n:(i + 1) * n],
                        lhsT=xc[:, lo:lo + 128].bitcast(FP8X4),
                        lhsT_scale=xs[:, lo:lo + 128],
                        rhs=pc[:, h, :].bitcast(FP8X4),
                        rhs_scale=ps[:, h, :],
                        start=(h == 0),
                        stop=(h == 1),
                    )
            nu = u1 - u0
            cuts = [q0] + [q for q in range(RING, NQ, RING) if q0 < q < q1] + [q1]
            use_v = stored > 0 and bi % 4 == 3
            for qa, qb in zip(cuts[:-1], cuts[1:]):
                a = off + (qa - q0) * d
                src = acc[:, 0:nu * n].rearrange("p (u n) -> p u n", n=n)[:, :, a:a + (qb - qa) * d]
                src = src.rearrange("p u (q m) -> p q u m", m=d)
                r = qa % RING
                dst = ring[:, r * CP:(r + qb - qa) * CP].rearrange("p (q c) -> p q c", c=CP)
                dst = dst[:, :, cl + u0 * d:cl + u1 * d].rearrange("p q (u m) -> p q u m", m=d)
                if use_v:
                    nc.vector.tensor_scalar_mul(out=dst, in0=src, scalar1=SCALE)
                else:
                    nc.scalar.activation(out=dst, in_=src, func=mybir.ActivationFunctionType.Copy, scale=SCALE)
            if u1 == d and (fin - stored >= STORE or fin == NQ):
                cuts = [stored] + [q for q in range(RING, NQ, RING) if stored < q < fin] + [fin]
                for qa, qb in zip(cuts[:-1], cuts[1:]):
                    r = qa % RING
                    nc.sync.dma_start(
                        out=out_v[:, qa:qb, :],
                        in_=ring[:, r * CP:(r + qb - qa) * CP].rearrange("p (q c) -> p q c", c=CP)[:, :, 0:C],
                    )
                stored = fin
